import numpy as np
import ml_dtypes


def mxq(x, axis, fmt="e4m3"):
    dtype, down = {"e4m3": (ml_dtypes.float8_e4m3fn, 7), "e5m2": (ml_dtypes.float8_e5m2, 14)}[fmt]
    v = np.moveaxis(np.asarray(x, np.float32).astype(ml_dtypes.bfloat16).astype(np.float64), axis, -1)
    blocks = v.reshape(v.shape[:-1] + (-1, 32))
    amax = np.abs(blocks).max(-1, keepdims=True)
    byte = np.maximum(np.where(amax > 0, np.frexp(amax)[1] - 1 + 127, 0) - down, 1)
    scale = np.exp2(byte - 127.0)
    codes = (blocks / scale).astype(np.float32).astype(dtype).astype(np.float64)
    return np.moveaxis((codes * scale).reshape(v.shape), -1, axis)


WIDE = False


def mx_kscale(k):
    if not WIDE:
        return np.ones(k)
    levels = np.array([10, -10, 5, -5, 0])
    a = np.random.permutation(np.resize(levels, k // 512 * 4)).reshape(k // 512, 4)
    idx = np.arange(k)
    return np.exp2(a[idx // 512, idx % 128 // 32])


BF16 = ml_dtypes.bfloat16


def bf(x):
    return np.asarray(x, np.float32).astype(BF16)


def f64(x):
    return np.asarray(x).astype(np.float64)


B, T, D, K = 4, 64, 8192, 512
N = B * T
DIST_SCALE = 400.0
SX = np.sqrt(5.0 * DIST_SCALE / D)


def setup_inputs():
    s = mx_kscale(D)
    s = s / np.sqrt(np.mean(s * s))
    return {
        "x": bf(np.random.standard_normal((N, D)) * SX * s),
        "logvar_W": bf(np.random.standard_normal((D, K)) * 0.08 / np.sqrt(D) / s[:, None]),
        "logvar_b": bf(np.random.standard_normal(K) * 0.1),
        "embedding": bf(np.random.standard_normal((K, D)) * SX),
    }


def reference(x, logvar_W, logvar_b, embedding):
    x, emb = f64(x), f64(embedding)
    xq = mxq(x, 1, "e4m3")
    z_logvar = (xq @ mxq(f64(logvar_W), 0, "e4m3")) + f64(logvar_b)
    distances = (
        np.sum(x * x, axis=1, keepdims=True)
        + np.sum(emb * emb, axis=1)
        - 2.0 * (xq @ mxq(emb, 1, "e4m3").T)
    )
    smooth = np.exp(-2.0 * z_logvar)
    d = distances / DIST_SCALE
    prob = np.exp(-d * (0.5 * smooth)) / np.sqrt(smooth)
    probs = prob / np.sum(prob, axis=1, keepdims=True)
    quantized = mxq(probs, 1, "e4m3") @ mxq(emb, 0, "e4m3")
    return quantized, probs

@@ -1,0 +1,355 @@
+from contextlib import ExitStack
+
+import concourse.mybir as mybir
+from concourse.masks import make_identity
+
+F32 = mybir.dt.float32
+BF16 = mybir.dt.bfloat16
+U32 = mybir.dt.uint32
+U8 = mybir.dt.uint8
+FP8X4 = mybir.dt.float8_e4m3fn_x4
+ACT = mybir.ActivationFunctionType
+ALU = mybir.AluOpType
+AX = mybir.AxisListType
+
+P = 128
+PACK = 4
+K_PASS = P * PACK
+TOKENS, FEATURES, CODES = 256, 8192, 512
+TOKEN_TILES = TOKENS // P
+CODE_TILES = CODES // P
+PASSES = FEATURES // K_PASS
+PAIRS = K_PASS // 2
+CHUNK = 1024
+CHUNKS = FEATURES // CHUNK
+PASSES_PER_CHUNK = CHUNK // K_PASS
+BANK = 512
+AHEAD = 2
+EARLY_BLOCKS = 10
+STORE_BLOCKS = 2
+DIST_SCALE = 400.0
+
+FLOPS = 3 * 2 * TOKENS * FEATURES * CODES
+
+
+def tile_vq_payam_gssoft_pa_k_kernel(tc, x, logvar_W, logvar_b, embedding, out_0, out_1):
+    nc = tc.nc
+
+    x_view = x.rearrange("(m p) f -> p m f", p=P)
+    emb_view = embedding.rearrange("(t p) f -> p t f", p=P)
+    w_view = logvar_W.rearrange("(s q e) n -> q s e n", q=P, e=2)
+
+    with ExitStack() as ctx:
+        consts = ctx.enter_context(tc.tile_pool(name="consts", bufs=1))
+        keep = ctx.enter_context(tc.tile_pool(name="keep", bufs=1))
+        by_code = ctx.enter_context(tc.tile_pool(name="by_code", bufs=2))
+        sums = ctx.enter_context(tc.psum_pool(name="sums", bufs=1))
+        banks = ctx.enter_context(tc.psum_pool(name="banks", bufs=4))
+
+        ident_f32 = consts.tile([P, P], F32)
+        make_identity(nc, ident_f32[:])
+        ident_bf16 = consts.tile([P, P], BF16)
+        make_identity(nc, ident_bf16[:])
+
+        warm_in = consts.tile([P, 1], F32)
+        nc.vector.memset(warm_in[:], 0.0)
+        warm_out = consts.tile([P, 1], F32)
+        nc.scalar.activation(out=warm_out[:], in_=warm_in[:], func=ACT.Exp)
+
+        ones = consts.tile([P, P], BF16)
+        nc.vector.memset(ones[:], 1.0)
+        bias_rows = consts.tile([P, CODES], BF16)
+        nc.vector.memset(bias_rows[:], 0.0)
+        nc.sync.dma_start(out=bias_rows[0:1, :], in_=logvar_b.rearrange("(o n) -> o n", o=1))
+        bias_bank = banks.tile([P, BANK], F32, tag="bank")
+        nc.tensor.matmul(out=bias_bank[:], lhsT=ones[:], rhs=bias_rows[:], start=True, stop=True)
+        bias_all = consts.tile([P, CODES], F32)
+        nc.vector.tensor_copy(out=bias_all[:], in_=bias_bank[:])
+
+        emb_sq_parts = consts.tile([P, CODE_TILES * CHUNKS], F32)
+        x_sq_parts = consts.tile([P, TOKEN_TILES * CHUNKS], F32)
+        emb_sq = consts.tile([P, CODE_TILES], F32)
+        x_sq = consts.tile([P, TOKEN_TILES], F32)
+        x_sq_scaled = consts.tile([P, TOKEN_TILES], F32)
+        emb_sq_repeated = consts.tile([P, CODE_TILES, P], F32)
+        emb_sq_scaled = consts.tile([P, CODES], F32)
+
+        raw_emb = {}
+        for c in range(CHUNKS):
+            raw_emb[c] = keep.tile([P, CODE_TILES * CHUNK], BF16, name="raw_emb%d" % c)
+        emb_by_code = keep.tile([P, FEATURES], U32, align_bytes=64)
+        emb_by_code_scales = keep.tile([P, FEATURES], U8, align_bytes=64)
+
+        z_sum = {}
+        xe_sum = {}
+        for m in range(TOKEN_TILES):
+            z_sum[m] = sums.tile([P, BANK], F32, name="z_sum%d" % m)
+            xe_sum[m] = sums.tile([P, BANK], F32, name="xe_sum%d" % m)
+
+        def quantise(codes, scales, grouped):
+            nc.vector.quantize_mx(out=codes.bitcast(FP8X4), scales=scales, in_=grouped)
+
+        def regroup(grouped, rows):
+            nc.vector.tensor_copy(
+                out=grouped.rearrange("p (c i t) -> p c t i", i=4, t=PACK),
+                in_=rows.rearrange("p t (c i) -> p c t i", i=4),
+            )
+
+        def regroup_emb_by_code(j):
+            c, part = divmod(j, PASSES_PER_CHUNK)
+            grouped = by_code.tile([P, K_PASS * PACK], BF16, name="grouped_by_code", align_bytes=64)
+            rows = raw_emb[c][:].rearrange("p (t f) -> p t f", t=CODE_TILES)
+            regroup(grouped[:], rows[:, :, part * K_PASS : (part + 1) * K_PASS])
+            return grouped
+
+        def quantise_emb_by_code(j, grouped):
+            cols = slice(j * K_PASS, (j + 1) * K_PASS)
+            quantise(emb_by_code[:, cols], emb_by_code_scales[:, cols], grouped[:])
+
+        with ExitStack() as stream:
+            x_pool = stream.enter_context(tc.tile_pool(name="x_pool", bufs=AHEAD + 1))
+            w_pool = stream.enter_context(tc.tile_pool(name="w_pool", bufs=AHEAD + 1))
+            grouped_pool = stream.enter_context(tc.tile_pool(name="grouped_pool", bufs=2))
+            codes_pool = stream.enter_context(tc.tile_pool(name="codes_pool", bufs=3))
+            unread = stream.enter_context(tc.tile_pool(name="unread", bufs=2))
+
+            raw_x = {}
+            raw_w = {}
+            turned = {}
+            operands = {}
+
+            def load_chunk(c):
+                cols = slice(c * CHUNK, (c + 1) * CHUNK)
+                raw_x[c] = x_pool.tile([P, TOKEN_TILES * CHUNK], BF16, name="raw_x")
+                nc.sync.dma_start(
+                    out=raw_x[c][:].rearrange("p (m f) -> p m f", m=TOKEN_TILES), in_=x_view[:, :, cols]
+                )
+                raw_w[c] = w_pool.tile([P, PASSES_PER_CHUNK * PACK * CODES], BF16, name="raw_w")
+                halves = slice(c * 2 * PASSES_PER_CHUNK, (c + 1) * 2 * PASSES_PER_CHUNK)
+                nc.sync.dma_start(
+                    out=raw_w[c][:].rearrange("p (s e n) -> p s e n", e=2, n=CODES),
+                    in_=w_view[:, halves, :, :],
+                )
+                nc.sync.dma_start(
+                    out=raw_emb[c][:].rearrange("p (t f) -> p t f", t=CODE_TILES), in_=emb_view[:, :, cols]
+                )
+
+            def square_rows(k):
+                c, half = divmod(k, 2)
+                rows = [(raw_x[c], half, x_sq_parts, half * CHUNKS + c)]
+                for t in (2 * half, 2 * half + 1):
+                    rows.append((raw_emb[c], t, emb_sq_parts, t * CHUNKS + c))
+                for raw, r, parts, col in rows:
+                    squares = unread.tile([P, CHUNK], BF16, name="squares")
+                    nc.scalar.activation(
+                        out=squares[:],
+                        in_=raw[:, r * CHUNK : (r + 1) * CHUNK],
+                        func=ACT.Square,
+                        accum_out=parts[:, col : col + 1],
+                    )
+
+            def transpose_pass(g):
+                c, part = divmod(g, PASSES_PER_CHUNK)
+                turned[g] = []
+                for raw, first_tile in ((raw_x[c], 0), (raw_emb[c], 0), (raw_emb[c], 2)):
+                    words = raw[:].bitcast(F32)
+                    bank = banks.tile([P, BANK], F32, tag="bank", name="turned")
+                    for i in range(2):
+                        for u in range(2):
+                            col = (first_tile + i) * (CHUNK // 2) + part * PAIRS + u * P
+                            nc.tensor.transpose(
+                                out=bank[:, (2 * i + u) * P : (2 * i + u + 1) * P],
+                                in_=words[:, col : col + P],
+                                identity=ident_f32[:],
+                            )
+                    turned[g].append(bank)
+
+            def interleave(engine_copy, grouped_words, bank):
+                engine_copy(
+                    out=grouped_words.rearrange("p (i r u) -> p i r u", i=2, u=2),
+                    in_=bank[:].rearrange("p (i u r) -> p i r u", i=2, u=2),
+                )
+
+            def quantise_pass(g):
+                c, part = divmod(g, PASSES_PER_CHUNK)
+                x_bank, emb_bank_0, emb_bank_1 = turned[g]
+                grouped_x = grouped_pool.tile([P, TOKENS * PACK], BF16, align_bytes=64)
+                interleave(nc.vector.tensor_copy, grouped_x[:].bitcast(F32), x_bank)
+                grouped_emb = grouped_pool.tile([P, CODES * PACK], BF16, align_bytes=64)
+                emb_words = grouped_emb[:].bitcast(F32)
+                interleave(nc.scalar.copy, emb_words[:, 0:BANK], emb_bank_0)
+                interleave(nc.scalar.copy, emb_words[:, BANK : 2 * BANK], emb_bank_1)
+                if g + 1 < PASSES:
+                    square_rows(g + 1)
+
+                grouped_w = grouped_pool.tile([P, CODES * PACK], BF16, align_bytes=64)
+                w_rows = raw_w[c][:].rearrange("p (g t n) -> p g t n", t=PACK, n=CODES)
+                regroup(grouped_w[:], w_rows[:, part, :, :])
+                if g < EARLY_BLOCKS:
+                    grouped_by_code = regroup_emb_by_code(g)
+
+                x_codes = codes_pool.tile([P, TOKENS], U32, align_bytes=64)
+                x_scales = codes_pool.tile([P, TOKENS], U8, align_bytes=64)
+                quantise(x_codes[:], x_scales[:], grouped_x[:])
+                w_codes = codes_pool.tile([P, CODES], U32, align_bytes=64)
+                w_scales = codes_pool.tile([P, CODES], U8, align_bytes=64)
+                quantise(w_codes[:], w_scales[:], grouped_w[:])
+                if g < EARLY_BLOCKS:
+                    quantise_emb_by_code(g, grouped_by_code)
+                emb_codes = codes_pool.tile([P, CODES], U32, align_bytes=64)
+                emb_scales = codes_pool.tile([P, CODES], U8, align_bytes=64)
+                quantise(emb_codes[:], emb_scales[:], grouped_emb[:])
+                operands[g] = (x_codes, x_scales, w_codes, w_scales, emb_codes, emb_scales)
+
+            def multiply_pass(g):
+                x_codes, x_scales, w_codes, w_scales, emb_codes, emb_scales = operands[g]
+                for m in range(TOKEN_TILES):
+                    tokens = slice(m * P, (m + 1) * P)
+                    for total, codes, scales in (
+                        (z_sum[m], w_codes, w_scales),
+                        (xe_sum[m], emb_codes, emb_scales),
+                    ):
+                        nc.tensor.matmul_mx(
+                            out=total[:],
+                            lhsT=x_codes[:, tokens].bitcast(FP8X4),
+                            lhsT_scale=x_scales[:, tokens],
+                            rhs=codes[:].bitcast(FP8X4),
+                            rhs_scale=scales[:],
+                            start=(g == 0),
+                            stop=(g == PASSES - 1),
+                        )
+
+            for c in range(AHEAD):
+                load_chunk(c)
+            square_rows(0)
+            transpose_pass(0)
+            for g in range(PASSES):
+                c, part = divmod(g, PASSES_PER_CHUNK)
+                if part == 0 and c + AHEAD < CHUNKS:
+                    load_chunk(c + AHEAD)
+                if g > 0:
+                    multiply_pass(g - 1)
+                if g + 1 < PASSES:
+                    transpose_pass(g + 1)
+                quantise_pass(g)
+
+            nc.vector.tensor_reduce(
+                out=emb_sq[:],
+                in_=emb_sq_parts[:].rearrange("p (t c) -> p t c", t=CODE_TILES),
+                axis=AX.X,
+                op=ALU.add,
+            )
+            nc.vector.tensor_reduce(
+                out=x_sq[:],
+                in_=x_sq_parts[:].rearrange("p (m c) -> p m c", m=TOKEN_TILES),
+                axis=AX.X,
+                op=ALU.add,
+            )
+            nc.vector.tensor_scalar(
+                out=x_sq_scaled[:], in0=x_sq[:], scalar1=0.5 / DIST_SCALE, scalar2=None, op0=ALU.mult
+            )
+            nc.vector.tensor_copy(
+                out=emb_sq_repeated[:], in_=emb_sq[:].unsqueeze(2).to_broadcast([P, CODE_TILES, P])
+            )
+            emb_sq_bank = banks.tile([P, BANK], F32, tag="bank")
+            for t in range(CODE_TILES):
+                nc.tensor.transpose(
+                    out=emb_sq_bank[:, t * P : (t + 1) * P], in_=emb_sq_repeated[:, t, :], identity=ident_f32[:]
+                )
+            nc.vector.tensor_scalar(
+                out=emb_sq_scaled[:], in0=emb_sq_bank[:], scalar1=0.5 / DIST_SCALE, scalar2=None, op0=ALU.mult
+            )
+
+            multiply_pass(PASSES - 1)
+
+        soft = ctx.enter_context(tc.tile_pool(name="soft", bufs=2))
+        results = ctx.enter_context(tc.tile_pool(name="results", bufs=3))
+
+        probs_codes = {}
+        probs_scales = {}
+        for m in range(TOKEN_TILES):
+            tokens = slice(m * P, (m + 1) * P)
+            zl = soft.tile([P, CODES], F32)
+            nc.vector.tensor_tensor(out=zl[:], in0=z_sum[m][:], in1=bias_all[:], op=ALU.add)
+            smooth = soft.tile([P, CODES], F32)
+            nc.scalar.activation(out=smooth[:], in_=zl[:], func=ACT.Exp, scale=-2.0)
+            part_dist = soft.tile([P, CODES], F32)
+            nc.vector.scalar_tensor_tensor(
+                out=part_dist[:],
+                in0=xe_sum[m][:],
+                scalar=-1.0 / DIST_SCALE,
+                in1=emb_sq_scaled[:],
+                op0=ALU.mult,
+                op1=ALU.add,
+            )
+            weighted = soft.tile([P, CODES], F32)
+            nc.vector.scalar_tensor_tensor(
+                out=weighted[:],
+                in0=part_dist[:],
+                scalar=x_sq_scaled[:, m : m + 1],
+                in1=smooth[:],
+                op0=ALU.add,
+                op1=ALU.mult,
+            )
+            neg_logit = soft.tile([P, CODES], F32)
+            nc.vector.tensor_tensor(out=neg_logit[:], in0=weighted[:], in1=zl[:], op=ALU.subtract)
+            neg_top = soft.tile([P, 1], F32)
+            nc.vector.tensor_reduce(out=neg_top[:], in_=neg_logit[:], axis=AX.X, op=ALU.min)
+            prob = soft.tile([P, CODES], F32)
+            row_sum = soft.tile([P, 1], F32)
+            nc.scalar.activation(
+                out=prob[:], in_=neg_logit[:], func=ACT.Exp, scale=-1.0, bias=neg_top[:], accum_out=row_sum[:]
+            )
+            inv_sum = soft.tile([P, 1], F32)
+            nc.vector.reciprocal(out=inv_sum[:], in_=row_sum[:])
+            probs_bf16 = soft.tile([P, CODES], BF16)
+            nc.scalar.activation(out=probs_bf16[:], in_=prob[:], func=ACT.Copy, scale=inv_sum[:])
+            probs = soft.tile([P, CODES], F32)
+            nc.vector.tensor_scalar(out=probs[:], in0=prob[:], scalar1=inv_sum[:], scalar2=None, op0=ALU.mult)
+            nc.sync.dma_start(out=out_1[tokens, :], in_=probs[:])
+
+            probs_bank = banks.tile([P, CODES], BF16, tag="bank")
+            for t in range(CODE_TILES):
+                nc.tensor.transpose(
+                    out=probs_bank[:, t * P : (t + 1) * P],
+                    in_=probs_bf16[:, t * P : (t + 1) * P],
+                    identity=ident_bf16[:],
+                )
+            grouped_probs = soft.tile([P, P * PACK], BF16, align_bytes=64)
+            nc.vector.tensor_copy(
+                out=grouped_probs[:].rearrange("p (r t) -> p r t", t=PACK),
+                in_=probs_bank[:].rearrange("p (t r) -> p r t", t=PACK),
+            )
+            probs_codes[m] = soft.tile([P, P], U32, name="probs_codes", align_bytes=64)
+            probs_scales[m] = soft.tile([P, P], U8, name="probs_scales", align_bytes=64)
+            quantise(probs_codes[m][:], probs_scales[m][:], grouped_probs[:])
+
+        result = {}
+        for j in range(PASSES):
+            if j >= EARLY_BLOCKS:
+                quantise_emb_by_code(j, regroup_emb_by_code(j))
+            cols = slice(j * K_PASS, (j + 1) * K_PASS)
+            place = j % STORE_BLOCKS
+            for m in range(TOKEN_TILES):
+                if place == 0:
+                    result[m] = results.tile([P, STORE_BLOCKS * BANK], F32, name="result%d" % m)
+                bank = banks.tile([P, BANK], F32, tag="bank", name="product")
+                nc.tensor.matmul_mx(
+                    out=bank[:],
+                    lhsT=probs_codes[m][:].bitcast(FP8X4),
+                    lhsT_scale=probs_scales[m][:],
+                    rhs=emb_by_code[:, cols].bitcast(FP8X4),
+                    rhs_scale=emb_by_code_scales[:, cols],
+                    start=True,
+                    stop=True,
+                )
+                target = result[m][:, place * BANK : (place + 1) * BANK]
+                if m == 1 and j < EARLY_BLOCKS:
+                    nc.vector.tensor_copy(out=target, in_=bank[:])
+                else:
+                    nc.scalar.copy(out=target, in_=bank[:])
+                if place == STORE_BLOCKS - 1:
+                    first = (j - place) * K_PASS
+                    nc.sync.dma_start(
+                        out=out_0[m * P : (m + 1) * P, first : first + STORE_BLOCKS * BANK], in_=result[m][:]
+                    )

@@ -25,9 +25,10 @@ CHUNKS = FEATURES // CHUNK
 PASSES_PER_CHUNK = CHUNK // K_PASS
 BANK = 512
 AHEAD = 2
-EARLY_BLOCKS = 10
+EARLY_BLOCKS = 2
 STORE_BLOCKS = 2
 DIST_SCALE = 400.0
+GRAM_TILE = 1
 
 FLOPS = 3 * 2 * TOKENS * FEATURES * CODES
 
@@ -44,7 +45,7 @@ def tile_vq_payam_gssoft_pa_k_kernel(tc, x, logvar_W, logvar_b, embedding, out_0
         keep = ctx.enter_context(tc.tile_pool(name="keep", bufs=1))
         by_code = ctx.enter_context(tc.tile_pool(name="by_code", bufs=2))
         sums = ctx.enter_context(tc.psum_pool(name="sums", bufs=1))
-        banks = ctx.enter_context(tc.psum_pool(name="banks", bufs=4))
+        banks = ctx.enter_context(tc.psum_pool(name="banks", bufs=3))
 
         ident_f32 = consts.tile([P, P], F32)
         make_identity(nc, ident_f32[:])
@@ -67,7 +68,8 @@ def tile_vq_payam_gssoft_pa_k_kernel(tc, x, logvar_W, logvar_b, embedding, out_0
         nc.vector.tensor_copy(out=bias_all[:], in_=bias_bank[:])
 
         emb_sq_parts = consts.tile([P, CODE_TILES * CHUNKS], F32)
-        x_sq_parts = consts.tile([P, TOKEN_TILES * CHUNKS], F32)
+        x_sq_parts = consts.tile([P, CHUNKS], F32)
+        gram_diagonal = consts.tile([P, P], F32)
         emb_sq = consts.tile([P, CODE_TILES], F32)
         x_sq = consts.tile([P, TOKEN_TILES], F32)
         x_sq_scaled = consts.tile([P, TOKEN_TILES], F32)
@@ -85,6 +87,7 @@ def tile_vq_payam_gssoft_pa_k_kernel(tc, x, logvar_W, logvar_b, embedding, out_0
         for m in range(TOKEN_TILES):
             z_sum[m] = sums.tile([P, BANK], F32, name="z_sum%d" % m)
             xe_sum[m] = sums.tile([P, BANK], F32, name="xe_sum%d" % m)
+        gram = sums.tile([P, P], F32)
 
         def quantise(codes, scales, grouped):
             nc.vector.quantize_mx(out=codes.bitcast(FP8X4), scales=scales, in_=grouped)
@@ -118,25 +121,34 @@ def tile_vq_payam_gssoft_pa_k_kernel(tc, x, logvar_W, logvar_b, embedding, out_0
             turned = {}
             operands = {}
 
-            def load_chunk(c):
-                cols = slice(c * CHUNK, (c + 1) * CHUNK)
+            def load_chunk(c, pieces):
                 raw_x[c] = x_pool.tile([P, TOKEN_TILES * CHUNK], BF16, name="raw_x")
                 nc.sync.dma_start(
-                    out=raw_x[c][:].rearrange("p (m f) -> p m f", m=TOKEN_TILES), in_=x_view[:, :, cols]
+                    out=raw_x[c][:].rearrange("p (m f) -> p m f", m=TOKEN_TILES),
+                    in_=x_view[:, :, c * CHUNK : (c + 1) * CHUNK],
                 )
                 raw_w[c] = w_pool.tile([P, PASSES_PER_CHUNK * PACK * CODES], BF16, name="raw_w")
-                halves = slice(c * 2 * PASSES_PER_CHUNK, (c + 1) * 2 * PASSES_PER_CHUNK)
-                nc.sync.dma_start(
-                    out=raw_w[c][:].rearrange("p (s e n) -> p s e n", e=2, n=CODES),
-                    in_=w_view[:, halves, :, :],
-                )
-                nc.sync.dma_start(
-                    out=raw_emb[c][:].rearrange("p (t f) -> p t f", t=CODE_TILES), in_=emb_view[:, :, cols]
-                )
+                w_halves = raw_w[c][:].rearrange("p (s e n) -> p s e n", e=2, n=CODES)
+                emb_rows = raw_emb[c][:].rearrange("p (t f) -> p t f", t=CODE_TILES)
+                passes = PASSES_PER_CHUNK // pieces
+                for piece in range(pieces):
+                    first = piece * passes
+                    nc.sync.dma_start(
+                        out=w_halves[:, 2 * first : 2 * (first + passes), :, :],
+                        in_=w_view[
+                            :, 2 * (c * PASSES_PER_CHUNK + first) : 2 * (c * PASSES_PER_CHUNK + first + passes), :, :
+                        ],
+                    )
+                    nc.sync.dma_start(
+                        out=emb_rows[:, :, first * K_PASS : (first + passes) * K_PASS],
+                        in_=emb_view[:, :, c * CHUNK + first * K_PASS : c * CHUNK + (first + passes) * K_PASS],
+                    )
 
             def square_rows(k):
                 c, half = divmod(k, 2)
-                rows = [(raw_x[c], half, x_sq_parts, half * CHUNKS + c)]
+                rows = []
+                if half != GRAM_TILE:
+                    rows.append((raw_x[c], half, x_sq_parts, c))
                 for t in (2 * half, 2 * half + 1):
                     rows.append((raw_emb[c], t, emb_sq_parts, t * CHUNKS + c))
                 for raw, r, parts, col in rows:
@@ -173,11 +185,11 @@ def tile_vq_payam_gssoft_pa_k_kernel(tc, x, logvar_W, logvar_b, embedding, out_0
             def quantise_pass(g):
                 c, part = divmod(g, PASSES_PER_CHUNK)
                 x_bank, emb_bank_0, emb_bank_1 = turned[g]
-                grouped_x = grouped_pool.tile([P, TOKENS * PACK], BF16, align_bytes=64)
+                grouped_x = grouped_pool.tile([P, TOKENS * PACK], BF16, bufs=3, align_bytes=64)
                 interleave(nc.vector.tensor_copy, grouped_x[:].bitcast(F32), x_bank)
                 grouped_emb = grouped_pool.tile([P, CODES * PACK], BF16, align_bytes=64)
                 emb_words = grouped_emb[:].bitcast(F32)
-                interleave(nc.scalar.copy, emb_words[:, 0:BANK], emb_bank_0)
+                interleave(nc.vector.tensor_copy if g % 2 == 0 else nc.scalar.copy, emb_words[:, 0:BANK], emb_bank_0)
                 interleave(nc.scalar.copy, emb_words[:, BANK : 2 * BANK], emb_bank_1)
                 if g + 1 < PASSES:
                     square_rows(g + 1)
@@ -199,10 +211,10 @@ def tile_vq_payam_gssoft_pa_k_kernel(tc, x, logvar_W, logvar_b, embedding, out_0
                 emb_codes = codes_pool.tile([P, CODES], U32, align_bytes=64)
                 emb_scales = codes_pool.tile([P, CODES], U8, align_bytes=64)
                 quantise(emb_codes[:], emb_scales[:], grouped_emb[:])
-                operands[g] = (x_codes, x_scales, w_codes, w_scales, emb_codes, emb_scales)
+                operands[g] = (x_codes, x_scales, w_codes, w_scales, emb_codes, emb_scales, grouped_x)
 
             def multiply_pass(g):
-                x_codes, x_scales, w_codes, w_scales, emb_codes, emb_scales = operands[g]
+                x_codes, x_scales, w_codes, w_scales, emb_codes, emb_scales, grouped_x = operands[g]
                 for m in range(TOKEN_TILES):
                     tokens = slice(m * P, (m + 1) * P)
                     for total, codes, scales in (
@@ -218,15 +230,26 @@ def tile_vq_payam_gssoft_pa_k_kernel(tc, x, logvar_W, logvar_b, embedding, out_0
                             start=(g == 0),
                             stop=(g == PASSES - 1),
                         )
+                planes = grouped_x[:].rearrange("p (r t) -> p t r", t=PACK)
+                for t in range(PACK):
+                    plane = planes[:, t, GRAM_TILE * P : (GRAM_TILE + 1) * P]
+                    nc.tensor.matmul(
+                        out=gram[:],
+                        lhsT=plane,
+                        rhs=plane,
+                        start=(g == 0 and t == 0),
+                        stop=(g == PASSES - 1 and t == PACK - 1),
+                    )
 
-            for c in range(AHEAD):
-                load_chunk(c)
+            load_chunk(0, PASSES_PER_CHUNK)
+            for c in range(1, AHEAD):
+                load_chunk(c, 1)
             square_rows(0)
             transpose_pass(0)
             for g in range(PASSES):
                 c, part = divmod(g, PASSES_PER_CHUNK)
                 if part == 0 and c + AHEAD < CHUNKS:
-                    load_chunk(c + AHEAD)
+                    load_chunk(c + AHEAD, 1)
                 if g > 0:
                     multiply_pass(g - 1)
                 if g + 1 < PASSES:
@@ -239,14 +262,10 @@ def tile_vq_payam_gssoft_pa_k_kernel(tc, x, logvar_W, logvar_b, embedding, out_0
                 axis=AX.X,
                 op=ALU.add,
             )
-            nc.vector.tensor_reduce(
-                out=x_sq[:],
-                in_=x_sq_parts[:].rearrange("p (m c) -> p m c", m=TOKEN_TILES),
-                axis=AX.X,
-                op=ALU.add,
-            )
+            squared = slice(1 - GRAM_TILE, 2 - GRAM_TILE)
+            nc.vector.tensor_reduce(out=x_sq[:, squared], in_=x_sq_parts[:], axis=AX.X, op=ALU.add)
             nc.vector.tensor_scalar(
-                out=x_sq_scaled[:], in0=x_sq[:], scalar1=0.5 / DIST_SCALE, scalar2=None, op0=ALU.mult
+                out=x_sq_scaled[:, squared], in0=x_sq[:, squared], scalar1=0.5 / DIST_SCALE, scalar2=None, op0=ALU.mult
             )
             nc.vector.tensor_copy(
                 out=emb_sq_repeated[:], in_=emb_sq[:].unsqueeze(2).to_broadcast([P, CODE_TILES, P])
@@ -261,6 +280,13 @@ def tile_vq_payam_gssoft_pa_k_kernel(tc, x, logvar_W, logvar_b, embedding, out_0
             )
 
             multiply_pass(PASSES - 1)
+
+            by_gram = slice(GRAM_TILE, GRAM_TILE + 1)
+            nc.vector.tensor_tensor(out=gram_diagonal[:], in0=gram[:], in1=ident_f32[:], op=ALU.mult)
+            nc.vector.tensor_reduce(out=x_sq[:, by_gram], in_=gram_diagonal[:], axis=AX.X, op=ALU.add)
+            nc.vector.tensor_scalar(
+                out=x_sq_scaled[:, by_gram], in0=x_sq[:, by_gram], scalar1=0.5 / DIST_SCALE, scalar2=None, op0=ALU.mult
+            )
 
         soft = ctx.enter_context(tc.tile_pool(name="soft", bufs=2))
         results = ctx.enter_context(tc.tile_pool(name="results", bufs=3))
@@ -305,7 +331,7 @@ def tile_vq_payam_gssoft_pa_k_kernel(tc, x, logvar_W, logvar_b, embedding, out_0
             probs_bf16 = soft.tile([P, CODES], BF16)
             nc.scalar.activation(out=probs_bf16[:], in_=prob[:], func=ACT.Copy, scale=inv_sum[:])
             probs = soft.tile([P, CODES], F32)
-            nc.vector.tensor_scalar(out=probs[:], in0=prob[:], scalar1=inv_sum[:], scalar2=None, op0=ALU.mult)
+            nc.scalar.activation(out=probs[:], in_=prob[:], func=ACT.Copy, scale=inv_sum[:])
             nc.sync.dma_start(out=out_1[tokens, :], in_=probs[:])
 
             probs_bank = banks.tile([P, CODES], BF16, tag="bank")
@@ -316,7 +342,7 @@ def tile_vq_payam_gssoft_pa_k_kernel(tc, x, logvar_W, logvar_b, embedding, out_0
                     identity=ident_bf16[:],
                 )
             grouped_probs = soft.tile([P, P * PACK], BF16, align_bytes=64)
-            nc.vector.tensor_copy(
+            nc.scalar.copy(
                 out=grouped_probs[:].rearrange("p (r t) -> p r t", t=PACK),
                 in_=probs_bank[:].rearrange("p (t r) -> p r t", t=PACK),
             )
@@ -343,11 +369,7 @@ def tile_vq_payam_gssoft_pa_k_kernel(tc, x, logvar_W, logvar_b, embedding, out_0
                     start=True,
                     stop=True,
                 )
-                target = result[m][:, place * BANK : (place + 1) * BANK]
-                if m == 1 and j < EARLY_BLOCKS:
-                    nc.vector.tensor_copy(out=target, in_=bank[:])
-                else:
-                    nc.scalar.copy(out=target, in_=bank[:])
+                nc.scalar.copy(out=result[m][:, place * BANK : (place + 1) * BANK], in_=bank[:])
                 if place == STORE_BLOCKS - 1:
                     first = (j - place) * K_PASS
                     nc.sync.dma_start(

@@ -19,13 +19,14 @@ TOKENS, FEATURES, CODES = 256, 8192, 512
 TOKEN_TILES = TOKENS // P
 CODE_TILES = CODES // P
 PASSES = FEATURES // K_PASS
+BLOCKS = FEATURES // K_PASS
 PAIRS = K_PASS // 2
 CHUNK = 1024
 CHUNKS = FEATURES // CHUNK
 PASSES_PER_CHUNK = CHUNK // K_PASS
 BANK = 512
 AHEAD = 2
-EARLY_BLOCKS = 2
+EARLY_BLOCKS = BLOCKS // 2
 STORE_BLOCKS = 2
 DIST_SCALE = 400.0
 GRAM_TILE = 1
@@ -41,6 +42,7 @@ def tile_vq_payam_gssoft_pa_k_kernel(tc, x, logvar_W, logvar_b, embedding, out_0
     w_view = logvar_W.rearrange("(s q e) n -> q s e n", q=P, e=2)
 
     with ExitStack() as ctx:
+        ctx.enter_context(tc.manual_schedule())
         consts = ctx.enter_context(tc.tile_pool(name="consts", bufs=1))
         keep = ctx.enter_context(tc.tile_pool(name="keep", bufs=1))
         by_code = ctx.enter_context(tc.tile_pool(name="by_code", bufs=2))
@@ -112,45 +114,43 @@ def tile_vq_payam_gssoft_pa_k_kernel(tc, x, logvar_W, logvar_b, embedding, out_0
         with ExitStack() as stream:
             x_pool = stream.enter_context(tc.tile_pool(name="x_pool", bufs=AHEAD + 1))
             w_pool = stream.enter_context(tc.tile_pool(name="w_pool", bufs=AHEAD + 1))
-            grouped_pool = stream.enter_context(tc.tile_pool(name="grouped_pool", bufs=2))
+            grouped_pool = stream.enter_context(tc.tile_pool(name="grouped_pool", bufs=3))
             codes_pool = stream.enter_context(tc.tile_pool(name="codes_pool", bufs=3))
             unread = stream.enter_context(tc.tile_pool(name="unread", bufs=2))
 
             raw_x = {}
             raw_w = {}
             turned = {}
+            grouped_x = {}
+            grouped_emb = {}
             operands = {}
 
             def load_chunk(c, pieces):
                 raw_x[c] = x_pool.tile([P, TOKEN_TILES * CHUNK], BF16, name="raw_x")
-                nc.sync.dma_start(
-                    out=raw_x[c][:].rearrange("p (m f) -> p m f", m=TOKEN_TILES),
-                    in_=x_view[:, :, c * CHUNK : (c + 1) * CHUNK],
-                )
                 raw_w[c] = w_pool.tile([P, PASSES_PER_CHUNK * PACK * CODES], BF16, name="raw_w")
-                w_halves = raw_w[c][:].rearrange("p (s e n) -> p s e n", e=2, n=CODES)
+                x_rows = raw_x[c][:].rearrange("p (m f) -> p m f", m=TOKEN_TILES)
                 emb_rows = raw_emb[c][:].rearrange("p (t f) -> p t f", t=CODE_TILES)
+                w_halves = raw_w[c][:].rearrange("p (s e n) -> p s e n", e=2, n=CODES)
                 passes = PASSES_PER_CHUNK // pieces
                 for piece in range(pieces):
                     first = piece * passes
+                    here = slice(first * K_PASS, (first + passes) * K_PASS)
+                    there = slice(c * CHUNK + first * K_PASS, c * CHUNK + (first + passes) * K_PASS)
+                    nc.sync.dma_start(out=x_rows[:, :, here], in_=x_view[:, :, there])
+                    nc.sync.dma_start(out=emb_rows[:, :, here], in_=emb_view[:, :, there])
+                    g = c * PASSES_PER_CHUNK + first
                     nc.sync.dma_start(
                         out=w_halves[:, 2 * first : 2 * (first + passes), :, :],
-                        in_=w_view[
-                            :, 2 * (c * PASSES_PER_CHUNK + first) : 2 * (c * PASSES_PER_CHUNK + first + passes), :, :
-                        ],
-                    )
-                    nc.sync.dma_start(
-                        out=emb_rows[:, :, first * K_PASS : (first + passes) * K_PASS],
-                        in_=emb_view[:, :, c * CHUNK + first * K_PASS : c * CHUNK + (first + passes) * K_PASS],
+                        in_=w_view[:, 2 * g : 2 * (g + passes), :, :],
                     )
 
-            def square_rows(k):
-                c, half = divmod(k, 2)
-                rows = []
-                if half != GRAM_TILE:
-                    rows.append((raw_x[c], half, x_sq_parts, c))
-                for t in (2 * half, 2 * half + 1):
-                    rows.append((raw_emb[c], t, emb_sq_parts, t * CHUNKS + c))
+            def square_rows(g):
+                c, part = divmod(g, PASSES_PER_CHUNK)
+                if part == 0:
+                    rows = [(raw_emb[c], t, emb_sq_parts, t * CHUNKS + c) for t in range(CODE_TILES - 1)]
+                else:
+                    t = CODE_TILES - 1
+                    rows = [(raw_emb[c], t, emb_sq_parts, t * CHUNKS + c), (raw_x[c], 1 - GRAM_TILE, x_sq_parts, c)]
                 for raw, r, parts, col in rows:
                     squares = unread.tile([P, CHUNK], BF16, name="squares")
                     nc.scalar.activation(
@@ -182,39 +182,41 @@ def tile_vq_payam_gssoft_pa_k_kernel(tc, x, logvar_W, logvar_b, embedding, out_0
                     in_=bank[:].rearrange("p (i u r) -> p i r u", i=2, u=2),
                 )
 
+            def empty_banks(g):
+                x_bank, emb_bank_0, emb_bank_1 = turned[g]
+                grouped_x[g] = grouped_pool.tile([P, TOKENS * PACK], BF16, name="grouped_x", align_bytes=64)
+                interleave(nc.vector.tensor_copy, grouped_x[g][:].bitcast(F32), x_bank)
+                grouped_emb[g] = grouped_pool.tile([P, CODES * PACK], BF16, name="grouped_emb", align_bytes=64)
+                emb_words = grouped_emb[g][:].bitcast(F32)
+                interleave(nc.scalar.copy, emb_words[:, 0:BANK], emb_bank_0)
+                interleave(nc.scalar.copy, emb_words[:, BANK : 2 * BANK], emb_bank_1)
+
             def quantise_pass(g):
                 c, part = divmod(g, PASSES_PER_CHUNK)
-                x_bank, emb_bank_0, emb_bank_1 = turned[g]
-                grouped_x = grouped_pool.tile([P, TOKENS * PACK], BF16, bufs=3, align_bytes=64)
-                interleave(nc.vector.tensor_copy, grouped_x[:].bitcast(F32), x_bank)
-                grouped_emb = grouped_pool.tile([P, CODES * PACK], BF16, align_bytes=64)
-                emb_words = grouped_emb[:].bitcast(F32)
-                interleave(nc.vector.tensor_copy if g % 2 == 0 else nc.scalar.copy, emb_words[:, 0:BANK], emb_bank_0)
-                interleave(nc.scalar.copy, emb_words[:, BANK : 2 * BANK], emb_bank_1)
-                if g + 1 < PASSES:
-                    square_rows(g + 1)
-
+                early = g % 2 == 0 and g // 2 < EARLY_BLOCKS
+                if early:
+                    grouped_by_code = regroup_emb_by_code(g // 2)
                 grouped_w = grouped_pool.tile([P, CODES * PACK], BF16, align_bytes=64)
                 w_rows = raw_w[c][:].rearrange("p (g t n) -> p g t n", t=PACK, n=CODES)
                 regroup(grouped_w[:], w_rows[:, part, :, :])
-                if g < EARLY_BLOCKS:
-                    grouped_by_code = regroup_emb_by_code(g)
 
                 x_codes = codes_pool.tile([P, TOKENS], U32, align_bytes=64)
                 x_scales = codes_pool.tile([P, TOKENS], U8, align_bytes=64)
-                quantise(x_codes[:], x_scales[:], grouped_x[:])
+                quantise(x_codes[:], x_scales[:], grouped_x[g][:])
+                if early:
+                    quantise_emb_by_code(g // 2, grouped_by_code)
                 w_codes = codes_pool.tile([P, CODES], U32, align_bytes=64)
                 w_scales = codes_pool.tile([P, CODES], U8, align_bytes=64)
                 quantise(w_codes[:], w_scales[:], grouped_w[:])
-                if g < EARLY_BLOCKS:
-                    quantise_emb_by_code(g, grouped_by_code)
+                if g == PASSES - 1:
+                    spread_emb_squares()
                 emb_codes = codes_pool.tile([P, CODES], U32, align_bytes=64)
                 emb_scales = codes_pool.tile([P, CODES], U8, align_bytes=64)
-                quantise(emb_codes[:], emb_scales[:], grouped_emb[:])
-                operands[g] = (x_codes, x_scales, w_codes, w_scales, emb_codes, emb_scales, grouped_x)
+                quantise(emb_codes[:], emb_scales[:], grouped_emb[g][:])
+                operands[g] = (x_codes, x_scales, w_codes, w_scales, emb_codes, emb_scales)
 
             def multiply_pass(g):
-                x_codes, x_scales, w_codes, w_scales, emb_codes, emb_scales, grouped_x = operands[g]
+                x_codes, x_scales, w_codes, w_scales, emb_codes, emb_scales = operands[g]
                 for m in range(TOKEN_TILES):
                     tokens = slice(m * P, (m + 1) * P)
                     for total, codes, scales in (
@@ -230,7 +232,9 @@ def tile_vq_payam_gssoft_pa_k_kernel(tc, x, logvar_W, logvar_b, embedding, out_0
                             start=(g == 0),
                             stop=(g == PASSES - 1),
                         )
-                planes = grouped_x[:].rearrange("p (r t) -> p t r", t=PACK)
+
+            def gram_pass(g):
+                planes = grouped_x[g][:].rearrange("p (r t) -> p t r", t=PACK)
                 for t in range(PACK):
                     plane = planes[:, t, GRAM_TILE * P : (GRAM_TILE + 1) * P]
                     nc.tensor.matmul(
@@ -241,124 +245,132 @@ def tile_vq_payam_gssoft_pa_k_kernel(tc, x, logvar_W, logvar_b, embedding, out_0
                         stop=(g == PASSES - 1 and t == PACK - 1),
                     )
 
+            def spread_emb_squares():
+                nc.vector.tensor_reduce(
+                    out=emb_sq[:],
+                    in_=emb_sq_parts[:].rearrange("p (t c) -> p t c", t=CODE_TILES),
+                    axis=AX.X,
+                    op=ALU.add,
+                )
+                nc.vector.tensor_copy(
+                    out=emb_sq_repeated[:], in_=emb_sq[:].unsqueeze(2).to_broadcast([P, CODE_TILES, P])
+                )
+                emb_sq_bank = banks.tile([P, BANK], F32, tag="bank")
+                for t in range(CODE_TILES):
+                    nc.tensor.transpose(
+                        out=emb_sq_bank[:, t * P : (t + 1) * P],
+                        in_=emb_sq_repeated[:, t, :],
+                        identity=ident_f32[:],
+                    )
+                nc.scalar.mul(out=emb_sq_scaled[:], in_=emb_sq_bank[:], mul=0.5 / DIST_SCALE)
+
             load_chunk(0, PASSES_PER_CHUNK)
             for c in range(1, AHEAD):
                 load_chunk(c, 1)
-            square_rows(0)
             transpose_pass(0)
             for g in range(PASSES):
                 c, part = divmod(g, PASSES_PER_CHUNK)
                 if part == 0 and c + AHEAD < CHUNKS:
                     load_chunk(c + AHEAD, 1)
+                empty_banks(g)
                 if g > 0:
                     multiply_pass(g - 1)
                 if g + 1 < PASSES:
                     transpose_pass(g + 1)
+                if g > 0:
+                    gram_pass(g - 1)
+                square_rows(g)
                 quantise_pass(g)
-
-            nc.vector.tensor_reduce(
-                out=emb_sq[:],
-                in_=emb_sq_parts[:].rearrange("p (t c) -> p t c", t=CODE_TILES),
-                axis=AX.X,
-                op=ALU.add,
-            )
-            squared = slice(1 - GRAM_TILE, 2 - GRAM_TILE)
-            nc.vector.tensor_reduce(out=x_sq[:, squared], in_=x_sq_parts[:], axis=AX.X, op=ALU.add)
-            nc.vector.tensor_scalar(
-                out=x_sq_scaled[:, squared], in0=x_sq[:, squared], scalar1=0.5 / DIST_SCALE, scalar2=None, op0=ALU.mult
-            )
-            nc.vector.tensor_copy(
-                out=emb_sq_repeated[:], in_=emb_sq[:].unsqueeze(2).to_broadcast([P, CODE_TILES, P])
-            )
-            emb_sq_bank = banks.tile([P, BANK], F32, tag="bank")
-            for t in range(CODE_TILES):
-                nc.tensor.transpose(
-                    out=emb_sq_bank[:, t * P : (t + 1) * P], in_=emb_sq_repeated[:, t, :], identity=ident_f32[:]
-                )
-            nc.vector.tensor_scalar(
-                out=emb_sq_scaled[:], in0=emb_sq_bank[:], scalar1=0.5 / DIST_SCALE, scalar2=None, op0=ALU.mult
-            )
-
             multiply_pass(PASSES - 1)
+            gram_pass(PASSES - 1)
 
-            by_gram = slice(GRAM_TILE, GRAM_TILE + 1)
-            nc.vector.tensor_tensor(out=gram_diagonal[:], in0=gram[:], in1=ident_f32[:], op=ALU.mult)
-            nc.vector.tensor_reduce(out=x_sq[:, by_gram], in_=gram_diagonal[:], axis=AX.X, op=ALU.add)
-            nc.vector.tensor_scalar(
-                out=x_sq_scaled[:, by_gram], in0=x_sq[:, by_gram], scalar1=0.5 / DIST_SCALE, scalar2=None, op0=ALU.mult
-            )
+        soft = ctx.enter_context(tc.tile_pool(name="soft", bufs=2, reuse_waits="tile"))
+        results = ctx.enter_context(tc.tile_pool(name="results", bufs=4, reuse_waits="tile"))
 
-        soft = ctx.enter_context(tc.tile_pool(name="soft", bufs=2))
-        results = ctx.enter_context(tc.tile_pool(name="results", bufs=3))
+        zl, smooth, part_dist, neg_logit, neg_top, prob, row_sum = {}, {}, {}, {}, {}, {}, {}
+        probs_bf16, grouped_probs, probs_codes, probs_scales = {}, {}, {}, {}
 
-        probs_codes = {}
-        probs_scales = {}
-        for m in range(TOKEN_TILES):
-            tokens = slice(m * P, (m + 1) * P)
-            zl = soft.tile([P, CODES], F32)
-            nc.vector.tensor_tensor(out=zl[:], in0=z_sum[m][:], in1=bias_all[:], op=ALU.add)
-            smooth = soft.tile([P, CODES], F32)
-            nc.scalar.activation(out=smooth[:], in_=zl[:], func=ACT.Exp, scale=-2.0)
-            part_dist = soft.tile([P, CODES], F32)
+        def start_logit(m):
+            zl[m] = soft.tile([P, CODES], F32, name="zl")
+            nc.vector.tensor_tensor(out=zl[m][:], in0=z_sum[m][:], in1=bias_all[:], op=ALU.add)
+            smooth[m] = soft.tile([P, CODES], F32, name="smooth")
+            nc.scalar.activation(out=smooth[m][:], in_=zl[m][:], func=ACT.Exp, scale=-2.0)
+            part_dist[m] = soft.tile([P, CODES], F32, name="part_dist")
             nc.vector.scalar_tensor_tensor(
-                out=part_dist[:],
+                out=part_dist[m][:],
                 in0=xe_sum[m][:],
                 scalar=-1.0 / DIST_SCALE,
                 in1=emb_sq_scaled[:],
                 op0=ALU.mult,
                 op1=ALU.add,
             )
+
+        def finish_logit(m):
+            own = slice(m, m + 1)
+            if m == GRAM_TILE:
+                nc.vector.tensor_tensor(out=gram_diagonal[:], in0=gram[:], in1=ident_f32[:], op=ALU.mult)
+                nc.vector.tensor_reduce(out=x_sq[:, own], in_=gram_diagonal[:], axis=AX.X, op=ALU.add)
+            else:
+                nc.vector.tensor_reduce(out=x_sq[:, own], in_=x_sq_parts[:], axis=AX.X, op=ALU.add)
+            nc.vector.tensor_scalar(
+                out=x_sq_scaled[:, own], in0=x_sq[:, own], scalar1=0.5 / DIST_SCALE, scalar2=None, op0=ALU.mult
+            )
             weighted = soft.tile([P, CODES], F32)
             nc.vector.scalar_tensor_tensor(
                 out=weighted[:],
-                in0=part_dist[:],
-                scalar=x_sq_scaled[:, m : m + 1],
-                in1=smooth[:],
+                in0=part_dist[m][:],
+                scalar=x_sq_scaled[:, own],
+                in1=smooth[m][:],
                 op0=ALU.add,
                 op1=ALU.mult,
             )
-            neg_logit = soft.tile([P, CODES], F32)
-            nc.vector.tensor_tensor(out=neg_logit[:], in0=weighted[:], in1=zl[:], op=ALU.subtract)
-            neg_top = soft.tile([P, 1], F32)
-            nc.vector.tensor_reduce(out=neg_top[:], in_=neg_logit[:], axis=AX.X, op=ALU.min)
-            prob = soft.tile([P, CODES], F32)
-            row_sum = soft.tile([P, 1], F32)
+            neg_logit[m] = soft.tile([P, CODES], F32, name="neg_logit")
+            nc.vector.tensor_tensor(out=neg_logit[m][:], in0=weighted[:], in1=zl[m][:], op=ALU.subtract)
+            neg_top[m] = soft.tile([P, 1], F32, name="neg_top")
+            nc.vector.tensor_reduce(out=neg_top[m][:], in_=neg_logit[m][:], axis=AX.X, op=ALU.min)
+            prob[m] = soft.tile([P, CODES], F32, name="prob")
+            row_sum[m] = soft.tile([P, 1], F32, name="row_sum")
             nc.scalar.activation(
-                out=prob[:], in_=neg_logit[:], func=ACT.Exp, scale=-1.0, bias=neg_top[:], accum_out=row_sum[:]
+                out=prob[m][:],
+                in_=neg_logit[m][:],
+                func=ACT.Exp,
+                scale=-1.0,
+                bias=neg_top[m][:],
+                accum_out=row_sum[m][:],
             )
-            inv_sum = soft.tile([P, 1], F32)
-            nc.vector.reciprocal(out=inv_sum[:], in_=row_sum[:])
-            probs_bf16 = soft.tile([P, CODES], BF16)
-            nc.scalar.activation(out=probs_bf16[:], in_=prob[:], func=ACT.Copy, scale=inv_sum[:])
-            probs = soft.tile([P, CODES], F32)
-            nc.scalar.activation(out=probs[:], in_=prob[:], func=ACT.Copy, scale=inv_sum[:])
-            nc.sync.dma_start(out=out_1[tokens, :], in_=probs[:])
 
+        def normalise(m):
+            inv_sum = soft.tile([P, 1], F32)
+            nc.vector.reciprocal(out=inv_sum[:], in_=row_sum[m][:])
+            probs_bf16[m] = soft.tile([P, CODES], BF16, name="probs_bf16")
+            nc.scalar.activation(out=probs_bf16[m][:], in_=prob[m][:], func=ACT.Copy, scale=inv_sum[:])
+            probs = soft.tile([P, CODES], F32)
+            nc.vector.tensor_scalar(out=probs[:], in0=prob[m][:], scalar1=inv_sum[:], scalar2=None, op0=ALU.mult)
+            nc.sync.dma_start(out=out_1[m * P : (m + 1) * P, :], in_=probs[:])
+
+        def turn_probs(m):
             probs_bank = banks.tile([P, CODES], BF16, tag="bank")
             for t in range(CODE_TILES):
                 nc.tensor.transpose(
                     out=probs_bank[:, t * P : (t + 1) * P],
-                    in_=probs_bf16[:, t * P : (t + 1) * P],
+                    in_=probs_bf16[m][:, t * P : (t + 1) * P],
                     identity=ident_bf16[:],
                 )
-            grouped_probs = soft.tile([P, P * PACK], BF16, align_bytes=64)
+            grouped_probs[m] = soft.tile([P, P * PACK], BF16, name="grouped_probs", align_bytes=64)
             nc.scalar.copy(
-                out=grouped_probs[:].rearrange("p (r t) -> p r t", t=PACK),
+                out=grouped_probs[m][:].rearrange("p (r t) -> p r t", t=PACK),
                 in_=probs_bank[:].rearrange("p (t r) -> p r t", t=PACK),
             )
+
+        def quantise_probs(m):
             probs_codes[m] = soft.tile([P, P], U32, name="probs_codes", align_bytes=64)
             probs_scales[m] = soft.tile([P, P], U8, name="probs_scales", align_bytes=64)
-            quantise(probs_codes[m][:], probs_scales[m][:], grouped_probs[:])
+            quantise(probs_codes[m][:], probs_scales[m][:], grouped_probs[m][:])
 
-        result = {}
-        for j in range(PASSES):
-            if j >= EARLY_BLOCKS:
-                quantise_emb_by_code(j, regroup_emb_by_code(j))
-            cols = slice(j * K_PASS, (j + 1) * K_PASS)
-            place = j % STORE_BLOCKS
-            for m in range(TOKEN_TILES):
-                if place == 0:
-                    result[m] = results.tile([P, STORE_BLOCKS * BANK], F32, name="result%d" % m)
+        def store_products(m, first_block):
+            result = results.tile([P, STORE_BLOCKS * BANK], F32)
+            for place in range(STORE_BLOCKS):
+                cols = slice((first_block + place) * K_PASS, (first_block + place + 1) * K_PASS)
                 bank = banks.tile([P, BANK], F32, tag="bank", name="product")
                 nc.tensor.matmul_mx(
                     out=bank[:],
@@ -369,9 +381,34 @@ def tile_vq_payam_gssoft_pa_k_kernel(tc, x, logvar_W, logvar_b, embedding, out_0
                     start=True,
                     stop=True,
                 )
-                nc.scalar.copy(out=result[m][:, place * BANK : (place + 1) * BANK], in_=bank[:])
-                if place == STORE_BLOCKS - 1:
-                    first = (j - place) * K_PASS
-                    nc.sync.dma_start(
-                        out=out_0[m * P : (m + 1) * P, first : first + STORE_BLOCKS * BANK], in_=result[m][:]
-                    )
+                nc.scalar.copy(out=result[:, place * BANK : (place + 1) * BANK], in_=bank[:])
+            nc.sync.dma_start(
+                out=out_0[m * P : (m + 1) * P, first_block * K_PASS : (first_block + STORE_BLOCKS) * K_PASS],
+                in_=result[:],
+            )
+
+        start_logit(0)
+        finish_logit(0)
+        start_logit(1)
+        normalise(0)
+        turn_probs(0)
+        finish_logit(1)
+        quantise_probs(0)
+
+        early_stores = list(range(0, EARLY_BLOCKS, STORE_BLOCKS))
+        store_products(0, early_stores[0])
+        normalise(1)
+        store_products(0, early_stores[1])
+        turn_probs(1)
+        quantise_emb_by_code(EARLY_BLOCKS, regroup_emb_by_code(EARLY_BLOCKS))
+        store_products(0, early_stores[2])
+        quantise_probs(1)
+        for first_block in early_stores[3:]:
+            store_products(0, first_block)
+        for j in range(EARLY_BLOCKS + 1, BLOCKS):
+            quantise_emb_by_code(j, regroup_emb_by_code(j))
+        for first_block in early_stores:
+            store_products(1, first_block)
+        for m in range(TOKEN_TILES):
+            for first_block in range(EARLY_BLOCKS, BLOCKS, STORE_BLOCKS):
+                store_products(m, first_block)

@@ -19,17 +19,16 @@ TOKENS, FEATURES, CODES = 256, 8192, 512
 TOKEN_TILES = TOKENS // P
 CODE_TILES = CODES // P
 PASSES = FEATURES // K_PASS
-BLOCKS = FEATURES // K_PASS
 PAIRS = K_PASS // 2
 CHUNK = 1024
 CHUNKS = FEATURES // CHUNK
 PASSES_PER_CHUNK = CHUNK // K_PASS
 BANK = 512
 AHEAD = 2
-EARLY_BLOCKS = BLOCKS // 2
+EARLY_BLOCKS = 2
 STORE_BLOCKS = 2
 DIST_SCALE = 400.0
-GRAM_TILE = 1
+SCALAR_EMPTIES_EVERY = 4
 
 FLOPS = 3 * 2 * TOKENS * FEATURES * CODES
 
@@ -42,12 +41,11 @@ def tile_vq_payam_gssoft_pa_k_kernel(tc, x, logvar_W, logvar_b, embedding, out_0
     w_view = logvar_W.rearrange("(s q e) n -> q s e n", q=P, e=2)
 
     with ExitStack() as ctx:
-        ctx.enter_context(tc.manual_schedule())
         consts = ctx.enter_context(tc.tile_pool(name="consts", bufs=1))
         keep = ctx.enter_context(tc.tile_pool(name="keep", bufs=1))
         by_code = ctx.enter_context(tc.tile_pool(name="by_code", bufs=2))
         sums = ctx.enter_context(tc.psum_pool(name="sums", bufs=1))
-        banks = ctx.enter_context(tc.psum_pool(name="banks", bufs=3))
+        banks = ctx.enter_context(tc.psum_pool(name="banks", bufs=2))
 
         ident_f32 = consts.tile([P, P], F32)
         make_identity(nc, ident_f32[:])
@@ -70,8 +68,7 @@ def tile_vq_payam_gssoft_pa_k_kernel(tc, x, logvar_W, logvar_b, embedding, out_0
         nc.vector.tensor_copy(out=bias_all[:], in_=bias_bank[:])
 
         emb_sq_parts = consts.tile([P, CODE_TILES * CHUNKS], F32)
-        x_sq_parts = consts.tile([P, CHUNKS], F32)
-        gram_diagonal = consts.tile([P, P], F32)
+        gram_diagonal = consts.tile([P, TOKEN_TILES, P], F32)
         emb_sq = consts.tile([P, CODE_TILES], F32)
         x_sq = consts.tile([P, TOKEN_TILES], F32)
         x_sq_scaled = consts.tile([P, TOKEN_TILES], F32)
@@ -86,10 +83,13 @@ def tile_vq_payam_gssoft_pa_k_kernel(tc, x, logvar_W, logvar_b, embedding, out_0
 
         z_sum = {}
         xe_sum = {}
+        gram = {}
+        sum_tags = []
         for m in range(TOKEN_TILES):
             z_sum[m] = sums.tile([P, BANK], F32, name="z_sum%d" % m)
             xe_sum[m] = sums.tile([P, BANK], F32, name="xe_sum%d" % m)
-        gram = sums.tile([P, P], F32)
+            gram[m] = sums.tile([P, P], F32, name="gram%d" % m)
+            sum_tags.extend(["z_sum%d" % m, "xe_sum%d" % m, "gram%d" % m])
 
         def quantise(codes, scales, grouped):
             nc.vector.quantize_mx(out=codes.bitcast(FP8X4), scales=scales, in_=grouped)
@@ -114,50 +114,47 @@ def tile_vq_payam_gssoft_pa_k_kernel(tc, x, logvar_W, logvar_b, embedding, out_0
         with ExitStack() as stream:
             x_pool = stream.enter_context(tc.tile_pool(name="x_pool", bufs=AHEAD + 1))
             w_pool = stream.enter_context(tc.tile_pool(name="w_pool", bufs=AHEAD + 1))
-            grouped_pool = stream.enter_context(tc.tile_pool(name="grouped_pool", bufs=3))
+            grouped_pool = stream.enter_context(tc.tile_pool(name="grouped_pool", bufs=2))
             codes_pool = stream.enter_context(tc.tile_pool(name="codes_pool", bufs=3))
             unread = stream.enter_context(tc.tile_pool(name="unread", bufs=2))
 
             raw_x = {}
             raw_w = {}
             turned = {}
-            grouped_x = {}
-            grouped_emb = {}
             operands = {}
 
             def load_chunk(c, pieces):
                 raw_x[c] = x_pool.tile([P, TOKEN_TILES * CHUNK], BF16, name="raw_x")
+                nc.sync.dma_start(
+                    out=raw_x[c][:].rearrange("p (m f) -> p m f", m=TOKEN_TILES),
+                    in_=x_view[:, :, c * CHUNK : (c + 1) * CHUNK],
+                )
                 raw_w[c] = w_pool.tile([P, PASSES_PER_CHUNK * PACK * CODES], BF16, name="raw_w")
-                x_rows = raw_x[c][:].rearrange("p (m f) -> p m f", m=TOKEN_TILES)
-                emb_rows = raw_emb[c][:].rearrange("p (t f) -> p t f", t=CODE_TILES)
                 w_halves = raw_w[c][:].rearrange("p (s e n) -> p s e n", e=2, n=CODES)
+                emb_rows = raw_emb[c][:].rearrange("p (t f) -> p t f", t=CODE_TILES)
                 passes = PASSES_PER_CHUNK // pieces
                 for piece in range(pieces):
                     first = piece * passes
-                    here = slice(first * K_PASS, (first + passes) * K_PASS)
-                    there = slice(c * CHUNK + first * K_PASS, c * CHUNK + (first + passes) * K_PASS)
-                    nc.sync.dma_start(out=x_rows[:, :, here], in_=x_view[:, :, there])
-                    nc.sync.dma_start(out=emb_rows[:, :, here], in_=emb_view[:, :, there])
-                    g = c * PASSES_PER_CHUNK + first
                     nc.sync.dma_start(
                         out=w_halves[:, 2 * first : 2 * (first + passes), :, :],
-                        in_=w_view[:, 2 * g : 2 * (g + passes), :, :],
+                        in_=w_view[
+                            :, 2 * (c * PASSES_PER_CHUNK + first) : 2 * (c * PASSES_PER_CHUNK + first + passes), :, :
+                        ],
+                    )
+                    nc.sync.dma_start(
+                        out=emb_rows[:, :, first * K_PASS : (first + passes) * K_PASS],
+                        in_=emb_view[:, :, c * CHUNK + first * K_PASS : c * CHUNK + (first + passes) * K_PASS],
                     )
 
-            def square_rows(g):
-                c, part = divmod(g, PASSES_PER_CHUNK)
-                if part == 0:
-                    rows = [(raw_emb[c], t, emb_sq_parts, t * CHUNKS + c) for t in range(CODE_TILES - 1)]
-                else:
-                    t = CODE_TILES - 1
-                    rows = [(raw_emb[c], t, emb_sq_parts, t * CHUNKS + c), (raw_x[c], 1 - GRAM_TILE, x_sq_parts, c)]
-                for raw, r, parts, col in rows:
+            def square_rows(k):
+                c, half = divmod(k, 2)
+                for t in (2 * half, 2 * half + 1):
                     squares = unread.tile([P, CHUNK], BF16, name="squares")
                     nc.scalar.activation(
                         out=squares[:],
-                        in_=raw[:, r * CHUNK : (r + 1) * CHUNK],
+                        in_=raw_emb[c][:, t * CHUNK : (t + 1) * CHUNK],
                         func=ACT.Square,
-                        accum_out=parts[:, col : col + 1],
+                        accum_out=emb_sq_parts[:, t * CHUNKS + c : t * CHUNKS + c + 1],
                     )
 
             def transpose_pass(g):
@@ -182,41 +179,40 @@ def tile_vq_payam_gssoft_pa_k_kernel(tc, x, logvar_W, logvar_b, embedding, out_0
                     in_=bank[:].rearrange("p (i u r) -> p i r u", i=2, u=2),
                 )
 
-            def empty_banks(g):
-                x_bank, emb_bank_0, emb_bank_1 = turned[g]
-                grouped_x[g] = grouped_pool.tile([P, TOKENS * PACK], BF16, name="grouped_x", align_bytes=64)
-                interleave(nc.vector.tensor_copy, grouped_x[g][:].bitcast(F32), x_bank)
-                grouped_emb[g] = grouped_pool.tile([P, CODES * PACK], BF16, name="grouped_emb", align_bytes=64)
-                emb_words = grouped_emb[g][:].bitcast(F32)
-                interleave(nc.scalar.copy, emb_words[:, 0:BANK], emb_bank_0)
-                interleave(nc.scalar.copy, emb_words[:, BANK : 2 * BANK], emb_bank_1)
-
             def quantise_pass(g):
                 c, part = divmod(g, PASSES_PER_CHUNK)
-                early = g % 2 == 0 and g // 2 < EARLY_BLOCKS
-                if early:
-                    grouped_by_code = regroup_emb_by_code(g // 2)
+                x_bank, emb_bank_0, emb_bank_1 = turned[g]
+                grouped_x = grouped_pool.tile([P, TOKENS * PACK], BF16, bufs=3, align_bytes=64)
+                scalar_turn = g % SCALAR_EMPTIES_EVERY == SCALAR_EMPTIES_EVERY - 1
+                interleave(nc.scalar.copy if scalar_turn else nc.vector.tensor_copy, grouped_x[:].bitcast(F32), x_bank)
+                grouped_emb = grouped_pool.tile([P, CODES * PACK], BF16, align_bytes=64)
+                emb_words = grouped_emb[:].bitcast(F32)
+                interleave(nc.scalar.copy, emb_words[:, 0:BANK], emb_bank_0)
+                interleave(nc.scalar.copy, emb_words[:, BANK : 2 * BANK], emb_bank_1)
+                if g + 1 < PASSES:
+                    square_rows(g + 1)
+
                 grouped_w = grouped_pool.tile([P, CODES * PACK], BF16, align_bytes=64)
                 w_rows = raw_w[c][:].rearrange("p (g t n) -> p g t n", t=PACK, n=CODES)
                 regroup(grouped_w[:], w_rows[:, part, :, :])
+                if g < EARLY_BLOCKS:
+                    grouped_by_code = regroup_emb_by_code(g)
 
                 x_codes = codes_pool.tile([P, TOKENS], U32, align_bytes=64)
                 x_scales = codes_pool.tile([P, TOKENS], U8, align_bytes=64)
-                quantise(x_codes[:], x_scales[:], grouped_x[g][:])
-                if early:
-                    quantise_emb_by_code(g // 2, grouped_by_code)
+                quantise(x_codes[:], x_scales[:], grouped_x[:])
                 w_codes = codes_pool.tile([P, CODES], U32, align_bytes=64)
                 w_scales = codes_pool.tile([P, CODES], U8, align_bytes=64)
                 quantise(w_codes[:], w_scales[:], grouped_w[:])
-                if g == PASSES - 1:
-                    spread_emb_squares()
+                if g < EARLY_BLOCKS:
+                    quantise_emb_by_code(g, grouped_by_code)
                 emb_codes = codes_pool.tile([P, CODES], U32, align_bytes=64)
                 emb_scales = codes_pool.tile([P, CODES], U8, align_bytes=64)
-                quantise(emb_codes[:], emb_scales[:], grouped_emb[g][:])
-                operands[g] = (x_codes, x_scales, w_codes, w_scales, emb_codes, emb_scales)
+                quantise(emb_codes[:], emb_scales[:], grouped_emb[:])
+                operands[g] = (x_codes, x_scales, w_codes, w_scales, emb_codes, emb_scales, grouped_x)
 
             def multiply_pass(g):
-                x_codes, x_scales, w_codes, w_scales, emb_codes, emb_scales = operands[g]
+                x_codes, x_scales, w_codes, w_scales, emb_codes, emb_scales, grouped_x = operands[g]
                 for m in range(TOKEN_TILES):
                     tokens = slice(m * P, (m + 1) * P)
                     for total, codes, scales in (
@@ -232,146 +228,133 @@ def tile_vq_payam_gssoft_pa_k_kernel(tc, x, logvar_W, logvar_b, embedding, out_0
                             start=(g == 0),
                             stop=(g == PASSES - 1),
                         )
-
-            def gram_pass(g):
-                planes = grouped_x[g][:].rearrange("p (r t) -> p t r", t=PACK)
-                for t in range(PACK):
-                    plane = planes[:, t, GRAM_TILE * P : (GRAM_TILE + 1) * P]
-                    nc.tensor.matmul(
-                        out=gram[:],
-                        lhsT=plane,
-                        rhs=plane,
-                        start=(g == 0 and t == 0),
-                        stop=(g == PASSES - 1 and t == PACK - 1),
-                    )
-
-            def spread_emb_squares():
-                nc.vector.tensor_reduce(
-                    out=emb_sq[:],
-                    in_=emb_sq_parts[:].rearrange("p (t c) -> p t c", t=CODE_TILES),
-                    axis=AX.X,
-                    op=ALU.add,
-                )
-                nc.vector.tensor_copy(
-                    out=emb_sq_repeated[:], in_=emb_sq[:].unsqueeze(2).to_broadcast([P, CODE_TILES, P])
-                )
-                emb_sq_bank = banks.tile([P, BANK], F32, tag="bank")
-                for t in range(CODE_TILES):
-                    nc.tensor.transpose(
-                        out=emb_sq_bank[:, t * P : (t + 1) * P],
-                        in_=emb_sq_repeated[:, t, :],
-                        identity=ident_f32[:],
-                    )
-                nc.scalar.mul(out=emb_sq_scaled[:], in_=emb_sq_bank[:], mul=0.5 / DIST_SCALE)
+                planes = grouped_x[:].rearrange("p (r t) -> p t r", t=PACK)
+                for m in range(TOKEN_TILES):
+                    for t in range(PACK):
+                        plane = planes[:, t, m * P : (m + 1) * P]
+                        nc.tensor.matmul(
+                            out=gram[m][:],
+                            lhsT=plane,
+                            rhs=plane,
+                            start=(g == 0 and t == 0),
+                            stop=(g == PASSES - 1 and t == PACK - 1),
+                        )
 
             load_chunk(0, PASSES_PER_CHUNK)
             for c in range(1, AHEAD):
                 load_chunk(c, 1)
+            square_rows(0)
             transpose_pass(0)
             for g in range(PASSES):
                 c, part = divmod(g, PASSES_PER_CHUNK)
                 if part == 0 and c + AHEAD < CHUNKS:
                     load_chunk(c + AHEAD, 1)
-                empty_banks(g)
                 if g > 0:
                     multiply_pass(g - 1)
                 if g + 1 < PASSES:
                     transpose_pass(g + 1)
-                if g > 0:
-                    gram_pass(g - 1)
-                square_rows(g)
                 quantise_pass(g)
+
+            nc.vector.tensor_reduce(
+                out=emb_sq[:],
+                in_=emb_sq_parts[:].rearrange("p (t c) -> p t c", t=CODE_TILES),
+                axis=AX.X,
+                op=ALU.add,
+            )
+            nc.vector.tensor_copy(
+                out=emb_sq_repeated[:], in_=emb_sq[:].unsqueeze(2).to_broadcast([P, CODE_TILES, P])
+            )
+            emb_sq_bank = banks.tile([P, BANK], F32, tag="bank")
+            for t in range(CODE_TILES):
+                nc.tensor.transpose(
+                    out=emb_sq_bank[:, t * P : (t + 1) * P], in_=emb_sq_repeated[:, t, :], identity=ident_f32[:]
+                )
+            nc.vector.tensor_scalar(
+                out=emb_sq_scaled[:], in0=emb_sq_bank[:], scalar1=0.5 / DIST_SCALE, scalar2=None, op0=ALU.mult
+            )
+
             multiply_pass(PASSES - 1)
-            gram_pass(PASSES - 1)
 
-        soft = ctx.enter_context(tc.tile_pool(name="soft", bufs=2, reuse_waits="tile"))
-        results = ctx.enter_context(tc.tile_pool(name="results", bufs=4, reuse_waits="tile"))
+            for m in range(TOKEN_TILES):
+                own = slice(m, m + 1)
+                nc.vector.tensor_tensor(out=gram_diagonal[:, m, :], in0=gram[m][:], in1=ident_f32[:], op=ALU.mult)
+                nc.vector.tensor_reduce(out=x_sq[:, own], in_=gram_diagonal[:, m, :], axis=AX.X, op=ALU.add)
+                nc.vector.tensor_scalar(
+                    out=x_sq_scaled[:, own], in0=x_sq[:, own], scalar1=0.5 / DIST_SCALE, scalar2=None, op0=ALU.mult
+                )
 
-        zl, smooth, part_dist, neg_logit, neg_top, prob, row_sum = {}, {}, {}, {}, {}, {}, {}
-        probs_bf16, grouped_probs, probs_codes, probs_scales = {}, {}, {}, {}
+        soft = ctx.enter_context(tc.tile_pool(name="soft", bufs=2))
+        results = ctx.enter_context(tc.tile_pool(name="results", bufs=3))
 
-        def start_logit(m):
-            zl[m] = soft.tile([P, CODES], F32, name="zl")
-            nc.vector.tensor_tensor(out=zl[m][:], in0=z_sum[m][:], in1=bias_all[:], op=ALU.add)
-            smooth[m] = soft.tile([P, CODES], F32, name="smooth")
-            nc.scalar.activation(out=smooth[m][:], in_=zl[m][:], func=ACT.Exp, scale=-2.0)
-            part_dist[m] = soft.tile([P, CODES], F32, name="part_dist")
+        probs_codes = {}
+        probs_scales = {}
+        for m in range(TOKEN_TILES):
+            tokens = slice(m * P, (m + 1) * P)
+            zl = soft.tile([P, CODES], F32)
+            nc.vector.tensor_tensor(out=zl[:], in0=z_sum[m][:], in1=bias_all[:], op=ALU.add)
+            smooth = soft.tile([P, CODES], F32)
+            nc.scalar.activation(out=smooth[:], in_=zl[:], func=ACT.Exp, scale=-2.0)
+            part_dist = soft.tile([P, CODES], F32)
             nc.vector.scalar_tensor_tensor(
-                out=part_dist[m][:],
+                out=part_dist[:],
                 in0=xe_sum[m][:],
                 scalar=-1.0 / DIST_SCALE,
                 in1=emb_sq_scaled[:],
                 op0=ALU.mult,
                 op1=ALU.add,
             )
-
-        def finish_logit(m):
-            own = slice(m, m + 1)
-            if m == GRAM_TILE:
-                nc.vector.tensor_tensor(out=gram_diagonal[:], in0=gram[:], in1=ident_f32[:], op=ALU.mult)
-                nc.vector.tensor_reduce(out=x_sq[:, own], in_=gram_diagonal[:], axis=AX.X, op=ALU.add)
-            else:
-                nc.vector.tensor_reduce(out=x_sq[:, own], in_=x_sq_parts[:], axis=AX.X, op=ALU.add)
-            nc.vector.tensor_scalar(
-                out=x_sq_scaled[:, own], in0=x_sq[:, own], scalar1=0.5 / DIST_SCALE, scalar2=None, op0=ALU.mult
-            )
             weighted = soft.tile([P, CODES], F32)
             nc.vector.scalar_tensor_tensor(
                 out=weighted[:],
-                in0=part_dist[m][:],
-                scalar=x_sq_scaled[:, own],
-                in1=smooth[m][:],
+                in0=part_dist[:],
+                scalar=x_sq_scaled[:, m : m + 1],
+                in1=smooth[:],
                 op0=ALU.add,
                 op1=ALU.mult,
             )
-            neg_logit[m] = soft.tile([P, CODES], F32, name="neg_logit")
-            nc.vector.tensor_tensor(out=neg_logit[m][:], in0=weighted[:], in1=zl[m][:], op=ALU.subtract)
-            neg_top[m] = soft.tile([P, 1], F32, name="neg_top")
-            nc.vector.tensor_reduce(out=neg_top[m][:], in_=neg_logit[m][:], axis=AX.X, op=ALU.min)
-            prob[m] = soft.tile([P, CODES], F32, name="prob")
-            row_sum[m] = soft.tile([P, 1], F32, name="row_sum")
+            neg_logit = soft.tile([P, CODES], F32)
+            nc.vector.tensor_tensor(out=neg_logit[:], in0=weighted[:], in1=zl[:], op=ALU.subtract)
+            neg_top = soft.tile([P, 1], F32)
+            nc.vector.tensor_reduce(out=neg_top[:], in_=neg_logit[:], axis=AX.X, op=ALU.min)
+            prob = soft.tile([P, CODES], F32)
+            row_sum = soft.tile([P, 1], F32)
             nc.scalar.activation(
-                out=prob[m][:],
-                in_=neg_logit[m][:],
-                func=ACT.Exp,
-                scale=-1.0,
-                bias=neg_top[m][:],
-                accum_out=row_sum[m][:],
+                out=prob[:], in_=neg_logit[:], func=ACT.Exp, scale=-1.0, bias=neg_top[:], accum_out=row_sum[:]
             )
-
-        def normalise(m):
             inv_sum = soft.tile([P, 1], F32)
-            nc.vector.reciprocal(out=inv_sum[:], in_=row_sum[m][:])
-            probs_bf16[m] = soft.tile([P, CODES], BF16, name="probs_bf16")
-            nc.scalar.activation(out=probs_bf16[m][:], in_=prob[m][:], func=ACT.Copy, scale=inv_sum[:])
+            nc.vector.reciprocal(out=inv_sum[:], in_=row_sum[:])
+            probs_bf16 = soft.tile([P, CODES], BF16)
+            nc.scalar.activation(out=probs_bf16[:], in_=prob[:], func=ACT.Copy, scale=inv_sum[:])
             probs = soft.tile([P, CODES], F32)
-            nc.vector.tensor_scalar(out=probs[:], in0=prob[m][:], scalar1=inv_sum[:], scalar2=None, op0=ALU.mult)
-            nc.sync.dma_start(out=out_1[m * P : (m + 1) * P, :], in_=probs[:])
+            nc.scalar.activation(out=probs[:], in_=prob[:], func=ACT.Copy, scale=inv_sum[:])
+            nc.sync.dma_start(out=out_1[tokens, :], in_=probs[:])
 
-        def turn_probs(m):
             probs_bank = banks.tile([P, CODES], BF16, tag="bank")
             for t in range(CODE_TILES):
                 nc.tensor.transpose(
                     out=probs_bank[:, t * P : (t + 1) * P],
-                    in_=probs_bf16[m][:, t * P : (t + 1) * P],
+                    in_=probs_bf16[:, t * P : (t + 1) * P],
                     identity=ident_bf16[:],
                 )
-            grouped_probs[m] = soft.tile([P, P * PACK], BF16, name="grouped_probs", align_bytes=64)
+            grouped_probs = soft.tile([P, P * PACK], BF16, align_bytes=64)
             nc.scalar.copy(
-                out=grouped_probs[m][:].rearrange("p (r t) -> p r t", t=PACK),
+                out=grouped_probs[:].rearrange("p (r t) -> p r t", t=PACK),
                 in_=probs_bank[:].rearrange("p (t r) -> p r t", t=PACK),
             )
-
-        def quantise_probs(m):
             probs_codes[m] = soft.tile([P, P], U32, name="probs_codes", align_bytes=64)
             probs_scales[m] = soft.tile([P, P], U8, name="probs_scales", align_bytes=64)
-            quantise(probs_codes[m][:], probs_scales[m][:], grouped_probs[m][:])
+            quantise(probs_codes[m][:], probs_scales[m][:], grouped_probs[:])
 
-        def store_products(m, first_block):
-            result = results.tile([P, STORE_BLOCKS * BANK], F32)
-            for place in range(STORE_BLOCKS):
-                cols = slice((first_block + place) * K_PASS, (first_block + place + 1) * K_PASS)
-                bank = banks.tile([P, BANK], F32, tag="bank", name="product")
+        result = {}
+        for j in range(PASSES):
+            if j >= EARLY_BLOCKS:
+                quantise_emb_by_code(j, regroup_emb_by_code(j))
+            cols = slice(j * K_PASS, (j + 1) * K_PASS)
+            place = j % STORE_BLOCKS
+            for m in range(TOKEN_TILES):
+                if place == 0:
+                    result[m] = results.tile([P, STORE_BLOCKS * BANK], F32, name="result%d" % m)
+                bank = sums.tile([P, BANK], F32, tag=sum_tags[(TOKEN_TILES * j + m) % len(sum_tags)], name="product")
                 nc.tensor.matmul_mx(
                     out=bank[:],
                     lhsT=probs_codes[m][:].bitcast(FP8X4),
@@ -381,34 +364,9 @@ def tile_vq_payam_gssoft_pa_k_kernel(tc, x, logvar_W, logvar_b, embedding, out_0
                     start=True,
                     stop=True,
                 )
-                nc.scalar.copy(out=result[:, place * BANK : (place + 1) * BANK], in_=bank[:])
-            nc.sync.dma_start(
-                out=out_0[m * P : (m + 1) * P, first_block * K_PASS : (first_block + STORE_BLOCKS) * K_PASS],
-                in_=result[:],
-            )
-
-        start_logit(0)
-        finish_logit(0)
-        start_logit(1)
-        normalise(0)
-        turn_probs(0)
-        finish_logit(1)
-        quantise_probs(0)
-
-        early_stores = list(range(0, EARLY_BLOCKS, STORE_BLOCKS))
-        store_products(0, early_stores[0])
-        normalise(1)
-        store_products(0, early_stores[1])
-        turn_probs(1)
-        quantise_emb_by_code(EARLY_BLOCKS, regroup_emb_by_code(EARLY_BLOCKS))
-        store_products(0, early_stores[2])
-        quantise_probs(1)
-        for first_block in early_stores[3:]:
-            store_products(0, first_block)
-        for j in range(EARLY_BLOCKS + 1, BLOCKS):
-            quantise_emb_by_code(j, regroup_emb_by_code(j))
-        for first_block in early_stores:
-            store_products(1, first_block)
-        for m in range(TOKEN_TILES):
-            for first_block in range(EARLY_BLOCKS, BLOCKS, STORE_BLOCKS):
-                store_products(m, first_block)
+                nc.scalar.copy(out=result[m][:, place * BANK : (place + 1) * BANK], in_=bank[:])
+                if place == STORE_BLOCKS - 1:
+                    first = (j - place) * K_PASS
+                    nc.sync.dma_start(
+                        out=out_0[m * P : (m + 1) * P, first : first + STORE_BLOCKS * BANK], in_=result[m][:]
+                    )

@@ -45,7 +45,7 @@ def tile_vq_payam_gssoft_pa_k_kernel(tc, x, logvar_W, logvar_b, embedding, out_0
         keep = ctx.enter_context(tc.tile_pool(name="keep", bufs=1))
         by_code = ctx.enter_context(tc.tile_pool(name="by_code", bufs=2))
         sums = ctx.enter_context(tc.psum_pool(name="sums", bufs=1))
-        banks = ctx.enter_context(tc.psum_pool(name="banks", bufs=2))
+        banks = ctx.enter_context(tc.psum_pool(name="banks", bufs=3))
 
         ident_f32 = consts.tile([P, P], F32)
         make_identity(nc, ident_f32[:])
@@ -70,7 +70,10 @@ def tile_vq_payam_gssoft_pa_k_kernel(tc, x, logvar_W, logvar_b, embedding, out_0
         emb_sq_parts = consts.tile([P, CODE_TILES * CHUNKS], F32)
         gram_diagonal = consts.tile([P, TOKEN_TILES, P], F32)
         emb_sq = consts.tile([P, CODE_TILES], F32)
-        x_sq = consts.tile([P, TOKEN_TILES], F32)
+        ident_scaled = consts.tile([P, P], F32)
+        nc.vector.tensor_scalar(
+            out=ident_scaled[:], in0=ident_f32[:], scalar1=0.5 / DIST_SCALE, scalar2=None, op0=ALU.mult
+        )
         x_sq_scaled = consts.tile([P, TOKEN_TILES], F32)
         emb_sq_repeated = consts.tile([P, CODE_TILES, P], F32)
         emb_sq_scaled = consts.tile([P, CODES], F32)
@@ -83,13 +86,15 @@ def tile_vq_payam_gssoft_pa_k_kernel(tc, x, logvar_W, logvar_b, embedding, out_0
 
         z_sum = {}
         xe_sum = {}
-        gram = {}
+        gram = sums.tile([P, TOKENS], F32, name="gram")
         sum_tags = []
         for m in range(TOKEN_TILES):
             z_sum[m] = sums.tile([P, BANK], F32, name="z_sum%d" % m)
             xe_sum[m] = sums.tile([P, BANK], F32, name="xe_sum%d" % m)
-            gram[m] = sums.tile([P, P], F32, name="gram%d" % m)
-            sum_tags.extend(["z_sum%d" % m, "xe_sum%d" % m, "gram%d" % m])
+            sum_tags.extend(["z_sum%d" % m, "xe_sum%d" % m])
+        sum_tags.append("gram")
+        zeros = consts.tile([P, TOKENS], BF16)
+        nc.vector.memset(zeros[:], 0.0)
 
         def quantise(codes, scales, grouped):
             nc.vector.quantize_mx(out=codes.bitcast(FP8X4), scales=scales, in_=grouped)
@@ -228,16 +233,18 @@ def tile_vq_payam_gssoft_pa_k_kernel(tc, x, logvar_W, logvar_b, embedding, out_0
                             start=(g == 0),
                             stop=(g == PASSES - 1),
                         )
+                if g == 0:
+                    nc.tensor.matmul(out=gram[:], lhsT=ones[:], rhs=zeros[:], start=True, stop=False)
                 planes = grouped_x[:].rearrange("p (r t) -> p t r", t=PACK)
                 for m in range(TOKEN_TILES):
                     for t in range(PACK):
                         plane = planes[:, t, m * P : (m + 1) * P]
                         nc.tensor.matmul(
-                            out=gram[m][:],
+                            out=gram[:, m * P : (m + 1) * P],
                             lhsT=plane,
                             rhs=plane,
-                            start=(g == 0 and t == 0),
-                            stop=(g == PASSES - 1 and t == PACK - 1),
+                            start=False,
+                            stop=(g == PASSES - 1 and m == TOKEN_TILES - 1 and t == PACK - 1),
                         )
 
             load_chunk(0, PASSES_PER_CHUNK)
@@ -275,13 +282,13 @@ def tile_vq_payam_gssoft_pa_k_kernel(tc, x, logvar_W, logvar_b, embedding, out_0
 
             multiply_pass(PASSES - 1)
 
-            for m in range(TOKEN_TILES):
-                own = slice(m, m + 1)
-                nc.vector.tensor_tensor(out=gram_diagonal[:, m, :], in0=gram[m][:], in1=ident_f32[:], op=ALU.mult)
-                nc.vector.tensor_reduce(out=x_sq[:, own], in_=gram_diagonal[:, m, :], axis=AX.X, op=ALU.add)
-                nc.vector.tensor_scalar(
-                    out=x_sq_scaled[:, own], in0=x_sq[:, own], scalar1=0.5 / DIST_SCALE, scalar2=None, op0=ALU.mult
-                )
+            nc.vector.tensor_tensor(
+                out=gram_diagonal[:],
+                in0=gram[:].rearrange("p (m n) -> p m n", m=TOKEN_TILES),
+                in1=ident_scaled[:].unsqueeze(1).to_broadcast([P, TOKEN_TILES, P]),
+                op=ALU.mult,
+            )
+            nc.vector.tensor_reduce(out=x_sq_scaled[:], in_=gram_diagonal[:], axis=AX.X, op=ALU.add)
 
         soft = ctx.enter_context(tc.tile_pool(name="soft", bufs=2))
         results = ctx.enter_context(tc.tile_pool(name="results", bufs=3))

@@ -25,10 +25,13 @@ CHUNKS = FEATURES // CHUNK
 PASSES_PER_CHUNK = CHUNK // K_PASS
 BANK = 512
 AHEAD = 2
-EARLY_BLOCKS = 2
+EARLY_BLOCKS = 6
+EARLY_EVERY = 2
+SINGLE_BLOCKS = 2
+VECTOR_BLOCKS = 2
 STORE_BLOCKS = 2
 DIST_SCALE = 400.0
-SCALAR_EMPTIES_EVERY = 4
+SCALAR_EMPTIES_EVERY = 2
 
 FLOPS = 3 * 2 * TOKENS * FEATURES * CODES
 
@@ -57,17 +60,9 @@ def tile_vq_payam_gssoft_pa_k_kernel(tc, x, logvar_W, logvar_b, embedding, out_0
         warm_out = consts.tile([P, 1], F32)
         nc.scalar.activation(out=warm_out[:], in_=warm_in[:], func=ACT.Exp)
 
-        ones = consts.tile([P, P], BF16)
-        nc.vector.memset(ones[:], 1.0)
-        bias_rows = consts.tile([P, CODES], BF16)
-        nc.vector.memset(bias_rows[:], 0.0)
-        nc.sync.dma_start(out=bias_rows[0:1, :], in_=logvar_b.rearrange("(o n) -> o n", o=1))
-        bias_bank = banks.tile([P, BANK], F32, tag="bank")
-        nc.tensor.matmul(out=bias_bank[:], lhsT=ones[:], rhs=bias_rows[:], start=True, stop=True)
-        bias_all = consts.tile([P, CODES], F32)
-        nc.vector.tensor_copy(out=bias_all[:], in_=bias_bank[:])
+        bias_all = consts.tile([P, CODES], BF16)
 
-        emb_sq_parts = consts.tile([P, CODE_TILES * CHUNKS], F32)
+        emb_sq_parts = consts.tile([P, CODE_TILES * (CHUNKS + 1)], F32)
         gram_diagonal = consts.tile([P, TOKEN_TILES, P], F32)
         emb_sq = consts.tile([P, CODE_TILES], F32)
         ident_scaled = consts.tile([P, P], F32)
@@ -75,12 +70,18 @@ def tile_vq_payam_gssoft_pa_k_kernel(tc, x, logvar_W, logvar_b, embedding, out_0
             out=ident_scaled[:], in0=ident_f32[:], scalar1=0.5 / DIST_SCALE, scalar2=None, op0=ALU.mult
         )
         x_sq_scaled = consts.tile([P, TOKEN_TILES], F32)
-        emb_sq_repeated = consts.tile([P, CODE_TILES, P], F32)
         emb_sq_scaled = consts.tile([P, CODES], F32)
 
         raw_emb = {}
+        emb_rows = {}
         for c in range(CHUNKS):
-            raw_emb[c] = keep.tile([P, CODE_TILES * CHUNK], BF16, name="raw_emb%d" % c)
+            parts = PASSES_PER_CHUNK if c == 0 else 1
+            for part in range(parts):
+                raw_emb[c, part] = keep.tile([P, CODE_TILES * CHUNK // parts], BF16, name="raw_emb%d_%d" % (c, part))
+            for part in range(PASSES_PER_CHUNK):
+                rows = raw_emb[c, part % parts][:].rearrange("p (t f) -> p t f", t=CODE_TILES)
+                first = (part // parts) * K_PASS
+                emb_rows[c * PASSES_PER_CHUNK + part] = rows[:, :, first : first + K_PASS]
         emb_by_code = keep.tile([P, FEATURES], U32, align_bytes=64)
         emb_by_code_scales = keep.tile([P, FEATURES], U8, align_bytes=64)
 
@@ -105,11 +106,9 @@ def tile_vq_payam_gssoft_pa_k_kernel(tc, x, logvar_W, logvar_b, embedding, out_0
                 in_=rows.rearrange("p t (c i) -> p c t i", i=4),
             )
 
-        def regroup_emb_by_code(j):
-            c, part = divmod(j, PASSES_PER_CHUNK)
-            grouped = by_code.tile([P, K_PASS * PACK], BF16, name="grouped_by_code", align_bytes=64)
-            rows = raw_emb[c][:].rearrange("p (t f) -> p t f", t=CODE_TILES)
-            regroup(grouped[:], rows[:, :, part * K_PASS : (part + 1) * K_PASS])
+        def regroup_emb_by_code(j, pool):
+            grouped = pool.tile([P, K_PASS * PACK], BF16, name="grouped_by_code", align_bytes=64)
+            regroup(grouped[:], emb_rows[j])
             return grouped
 
         def quantise_emb_by_code(j, grouped):
@@ -123,57 +122,67 @@ def tile_vq_payam_gssoft_pa_k_kernel(tc, x, logvar_W, logvar_b, embedding, out_0
             codes_pool = stream.enter_context(tc.tile_pool(name="codes_pool", bufs=3))
             unread = stream.enter_context(tc.tile_pool(name="unread", bufs=2))
 
-            raw_x = {}
+            x_rows = {}
             raw_w = {}
             turned = {}
             operands = {}
 
-            def load_chunk(c, pieces):
-                raw_x[c] = x_pool.tile([P, TOKEN_TILES * CHUNK], BF16, name="raw_x")
+            def load_x(c):
+                tile = x_pool.tile([P, TOKEN_TILES * CHUNK], BF16, name="raw_x")
+                rows = tile[:].rearrange("p (m f) -> p m f", m=TOKEN_TILES)
+                nc.sync.dma_start(out=rows, in_=x_view[:, :, c * CHUNK : (c + 1) * CHUNK])
+                for part in range(PASSES_PER_CHUNK):
+                    x_rows[c * PASSES_PER_CHUNK + part] = rows[:, :, part * K_PASS : (part + 1) * K_PASS]
+
+            def load_w(c, part, parts):
+                if part == 0:
+                    raw_w[c] = w_pool.tile([P, PASSES_PER_CHUNK * PACK * CODES], BF16, name="raw_w")
+                halves = raw_w[c][:].rearrange("p (s e n) -> p s e n", e=2, n=CODES)
+                count = 2 * PASSES_PER_CHUNK // parts
+                first = 2 * c * PASSES_PER_CHUNK + part * count
                 nc.sync.dma_start(
-                    out=raw_x[c][:].rearrange("p (m f) -> p m f", m=TOKEN_TILES),
-                    in_=x_view[:, :, c * CHUNK : (c + 1) * CHUNK],
+                    out=halves[:, part * count : (part + 1) * count, :, :], in_=w_view[:, first : first + count, :, :]
                 )
-                raw_w[c] = w_pool.tile([P, PASSES_PER_CHUNK * PACK * CODES], BF16, name="raw_w")
-                w_halves = raw_w[c][:].rearrange("p (s e n) -> p s e n", e=2, n=CODES)
-                emb_rows = raw_emb[c][:].rearrange("p (t f) -> p t f", t=CODE_TILES)
-                passes = PASSES_PER_CHUNK // pieces
-                for piece in range(pieces):
-                    first = piece * passes
-                    nc.sync.dma_start(
-                        out=w_halves[:, 2 * first : 2 * (first + passes), :, :],
-                        in_=w_view[
-                            :, 2 * (c * PASSES_PER_CHUNK + first) : 2 * (c * PASSES_PER_CHUNK + first + passes), :, :
-                        ],
-                    )
-                    nc.sync.dma_start(
-                        out=emb_rows[:, :, first * K_PASS : (first + passes) * K_PASS],
-                        in_=emb_view[:, :, c * CHUNK + first * K_PASS : c * CHUNK + (first + passes) * K_PASS],
-                    )
+
+            def load_emb(c, part, parts):
+                width = CHUNK // parts
+                first = c * CHUNK + part * width
+                nc.sync.dma_start(
+                    out=raw_emb[c, part][:].rearrange("p (t f) -> p t f", t=CODE_TILES),
+                    in_=emb_view[:, :, first : first + width],
+                )
+
+            def load_chunk(c):
+                load_x(c)
+                load_w(c, 0, 1)
+                load_emb(c, 0, 1)
 
             def square_rows(k):
                 c, half = divmod(k, 2)
-                for t in (2 * half, 2 * half + 1):
+                if c == 0:
+                    tile, width, tiles = raw_emb[0, half], K_PASS, range(CODE_TILES)
+                else:
+                    tile, width, tiles = raw_emb[c, 0], CHUNK, range(2 * half, 2 * half + 2)
+                for t in tiles:
                     squares = unread.tile([P, CHUNK], BF16, name="squares")
+                    column = t * (CHUNKS + 1) + (half if c == 0 else c + 1)
                     nc.scalar.activation(
-                        out=squares[:],
-                        in_=raw_emb[c][:, t * CHUNK : (t + 1) * CHUNK],
+                        out=squares[:, 0:width],
+                        in_=tile[:, t * width : (t + 1) * width],
                         func=ACT.Square,
-                        accum_out=emb_sq_parts[:, t * CHUNKS + c : t * CHUNKS + c + 1],
+                        accum_out=emb_sq_parts[:, column : column + 1],
                     )
 
             def transpose_pass(g):
-                c, part = divmod(g, PASSES_PER_CHUNK)
                 turned[g] = []
-                for raw, first_tile in ((raw_x[c], 0), (raw_emb[c], 0), (raw_emb[c], 2)):
-                    words = raw[:].bitcast(F32)
+                for rows, first_tile in ((x_rows[g], 0), (emb_rows[g], 0), (emb_rows[g], 2)):
                     bank = banks.tile([P, BANK], F32, tag="bank", name="turned")
                     for i in range(2):
+                        words = rows[:, first_tile + i, :].bitcast(F32)
                         for u in range(2):
-                            col = (first_tile + i) * (CHUNK // 2) + part * PAIRS + u * P
                             nc.tensor.transpose(
                                 out=bank[:, (2 * i + u) * P : (2 * i + u + 1) * P],
-                                in_=words[:, col : col + P],
+                                in_=words[:, u * P : (u + 1) * P],
                                 identity=ident_f32[:],
                             )
                     turned[g].append(bank)
@@ -184,57 +193,76 @@ def tile_vq_payam_gssoft_pa_k_kernel(tc, x, logvar_W, logvar_b, embedding, out_0
                     in_=bank[:].rearrange("p (i u r) -> p i r u", i=2, u=2),
                 )
 
-            def quantise_pass(g):
-                c, part = divmod(g, PASSES_PER_CHUNK)
+            def empty_banks(g):
                 x_bank, emb_bank_0, emb_bank_1 = turned[g]
                 grouped_x = grouped_pool.tile([P, TOKENS * PACK], BF16, bufs=3, align_bytes=64)
-                scalar_turn = g % SCALAR_EMPTIES_EVERY == SCALAR_EMPTIES_EVERY - 1
+                scalar_turn = g % SCALAR_EMPTIES_EVERY == 0
                 interleave(nc.scalar.copy if scalar_turn else nc.vector.tensor_copy, grouped_x[:].bitcast(F32), x_bank)
                 grouped_emb = grouped_pool.tile([P, CODES * PACK], BF16, align_bytes=64)
                 emb_words = grouped_emb[:].bitcast(F32)
                 interleave(nc.scalar.copy, emb_words[:, 0:BANK], emb_bank_0)
                 interleave(nc.scalar.copy, emb_words[:, BANK : 2 * BANK], emb_bank_1)
-                if g + 1 < PASSES:
-                    square_rows(g + 1)
+                return grouped_x, grouped_emb
 
+            def regroup_w(g):
+                c, part = divmod(g, PASSES_PER_CHUNK)
                 grouped_w = grouped_pool.tile([P, CODES * PACK], BF16, align_bytes=64)
                 w_rows = raw_w[c][:].rearrange("p (g t n) -> p g t n", t=PACK, n=CODES)
                 regroup(grouped_w[:], w_rows[:, part, :, :])
-                if g < EARLY_BLOCKS:
-                    grouped_by_code = regroup_emb_by_code(g)
+                return grouped_w
 
+            def quantise_x_and_w(grouped_x, grouped_w):
                 x_codes = codes_pool.tile([P, TOKENS], U32, align_bytes=64)
                 x_scales = codes_pool.tile([P, TOKENS], U8, align_bytes=64)
                 quantise(x_codes[:], x_scales[:], grouped_x[:])
                 w_codes = codes_pool.tile([P, CODES], U32, align_bytes=64)
                 w_scales = codes_pool.tile([P, CODES], U8, align_bytes=64)
                 quantise(w_codes[:], w_scales[:], grouped_w[:])
-                if g < EARLY_BLOCKS:
-                    quantise_emb_by_code(g, grouped_by_code)
+                return x_codes, x_scales, w_codes, w_scales
+
+            def quantise_emb(grouped_emb):
                 emb_codes = codes_pool.tile([P, CODES], U32, align_bytes=64)
                 emb_scales = codes_pool.tile([P, CODES], U8, align_bytes=64)
                 quantise(emb_codes[:], emb_scales[:], grouped_emb[:])
-                operands[g] = (x_codes, x_scales, w_codes, w_scales, emb_codes, emb_scales, grouped_x)
+                return emb_codes, emb_scales
+
+            def quantise_pass(g):
+                grouped_x, grouped_emb = empty_banks(g)
+                if g == 0:
+                    square_rows(0)
+                square_rows(g + 1)
+                grouped_w = regroup_w(g)
+                early = g % EARLY_EVERY == 0 and g // EARLY_EVERY < EARLY_BLOCKS
+                if early:
+                    grouped_by_code = regroup_emb_by_code(g // EARLY_EVERY, by_code)
+                codes = quantise_x_and_w(grouped_x, grouped_w)
+                if early:
+                    quantise_emb_by_code(g // EARLY_EVERY, grouped_by_code)
+                operands[g] = codes + quantise_emb(grouped_emb) + (grouped_x,)
+
+            def multiply(g, m, total, codes, scales):
+                x_codes, x_scales = operands[g][0:2]
+                tokens = slice(m * P, (m + 1) * P)
+                nc.tensor.matmul_mx(
+                    out=total[m][:],
+                    lhsT=x_codes[:, tokens].bitcast(FP8X4),
+                    lhsT_scale=x_scales[:, tokens],
+                    rhs=codes[:].bitcast(FP8X4),
+                    rhs_scale=scales[:],
+                    start=(g == 0),
+                    stop=(g == PASSES - 1),
+                )
 
             def multiply_pass(g):
-                x_codes, x_scales, w_codes, w_scales, emb_codes, emb_scales, grouped_x = operands[g]
+                w_codes, w_scales, emb_codes, emb_scales, grouped_x = operands[g][2:]
                 for m in range(TOKEN_TILES):
-                    tokens = slice(m * P, (m + 1) * P)
-                    for total, codes, scales in (
-                        (z_sum[m], w_codes, w_scales),
-                        (xe_sum[m], emb_codes, emb_scales),
-                    ):
-                        nc.tensor.matmul_mx(
-                            out=total[:],
-                            lhsT=x_codes[:, tokens].bitcast(FP8X4),
-                            lhsT_scale=x_scales[:, tokens],
-                            rhs=codes[:].bitcast(FP8X4),
-                            rhs_scale=scales[:],
-                            start=(g == 0),
-                            stop=(g == PASSES - 1),
-                        )
+                    multiply(g, m, z_sum, w_codes, w_scales)
+                    multiply(g, m, xe_sum, emb_codes, emb_scales)
+                add_gram(g, grouped_x)
+
+            def add_gram(g, grouped_x):
                 if g == 0:
-                    nc.tensor.matmul(out=gram[:], lhsT=ones[:], rhs=zeros[:], start=True, stop=False)
+                    nc.tensor.matmul(out=gram[:], lhsT=zeros[:, 0:P], rhs=zeros[:], start=True, stop=False)
                 planes = grouped_x[:].rearrange("p (r t) -> p t r", t=PACK)
                 for m in range(TOKEN_TILES):
                     for t in range(PACK):
@@ -247,133 +275,217 @@ def tile_vq_payam_gssoft_pa_k_kernel(tc, x, logvar_W, logvar_b, embedding, out_0
                             stop=(g == PASSES - 1 and m == TOKEN_TILES - 1 and t == PACK - 1),
                         )
 
-            load_chunk(0, PASSES_PER_CHUNK)
+            def sum_embedding_squares():
+                nc.vector.tensor_reduce(
+                    out=emb_sq[:],
+                    in_=emb_sq_parts[:].rearrange("p (t c) -> p t c", t=CODE_TILES),
+                    axis=AX.X,
+                    op=ALU.add,
+                )
+                emb_sq_bank = banks.tile([P, BANK], F32, tag="bank")
+                for t in range(CODE_TILES):
+                    nc.tensor.transpose(
+                        out=emb_sq_bank[:, t * P : (t + 1) * P],
+                        in_=emb_sq[:, t : t + 1].to_broadcast([P, P]),
+                        identity=ident_f32[:],
+                    )
+                nc.scalar.activation(out=emb_sq_scaled[:], in_=emb_sq_bank[:], func=ACT.Copy, scale=0.5 / DIST_SCALE)
+
+            load_x(0)
+            for part in range(PASSES_PER_CHUNK):
+                load_emb(0, part, PASSES_PER_CHUNK)
+                load_w(0, part, PASSES_PER_CHUNK)
             for c in range(1, AHEAD):
-                load_chunk(c, 1)
-            square_rows(0)
+                load_chunk(c)
             transpose_pass(0)
             for g in range(PASSES):
                 c, part = divmod(g, PASSES_PER_CHUNK)
                 if part == 0 and c + AHEAD < CHUNKS:
-                    load_chunk(c + AHEAD, 1)
+                    load_chunk(c + AHEAD)
+                    if c + AHEAD == CHUNKS - 1:
+                        nc.sync.dma_start(out=bias_all[:], in_=logvar_b.partition_broadcast(P))
                 if g > 0:
                     multiply_pass(g - 1)
                 if g + 1 < PASSES:
                     transpose_pass(g + 1)
-                quantise_pass(g)
+                if g < PASSES - 1:
+                    quantise_pass(g)
 
-            nc.vector.tensor_reduce(
-                out=emb_sq[:],
-                in_=emb_sq_parts[:].rearrange("p (t c) -> p t c", t=CODE_TILES),
-                axis=AX.X,
-                op=ALU.add,
-            )
-            nc.vector.tensor_copy(
-                out=emb_sq_repeated[:], in_=emb_sq[:].unsqueeze(2).to_broadcast([P, CODE_TILES, P])
-            )
-            emb_sq_bank = banks.tile([P, BANK], F32, tag="bank")
-            for t in range(CODE_TILES):
-                nc.tensor.transpose(
-                    out=emb_sq_bank[:, t * P : (t + 1) * P], in_=emb_sq_repeated[:, t, :], identity=ident_f32[:]
+            with tc.manual_schedule():
+                last = PASSES - 1
+                grouped_w = regroup_w(last)
+                grouped_x, grouped_emb = empty_banks(last)
+                operands[last] = quantise_x_and_w(grouped_x, grouped_w)
+                add_gram(last, grouped_x)
+                sum_embedding_squares()
+                for m in range(TOKEN_TILES):
+                    multiply(last, m, z_sum, *operands[last][2:4])
+                emb_operand = quantise_emb(grouped_emb)
+                for m in range(TOKEN_TILES):
+                    multiply(last, m, xe_sum, *emb_operand)
+                nc.vector.tensor_tensor(
+                    out=gram_diagonal[:],
+                    in0=gram[:].rearrange("p (m n) -> p m n", m=TOKEN_TILES),
+                    in1=ident_scaled[:].unsqueeze(1).to_broadcast([P, TOKEN_TILES, P]),
+                    op=ALU.mult,
                 )
-            nc.vector.tensor_scalar(
-                out=emb_sq_scaled[:], in0=emb_sq_bank[:], scalar1=0.5 / DIST_SCALE, scalar2=None, op0=ALU.mult
-            )
+                nc.vector.tensor_reduce(out=x_sq_scaled[:], in_=gram_diagonal[:], axis=AX.X, op=ALU.add)
 
-            multiply_pass(PASSES - 1)
-
-            nc.vector.tensor_tensor(
-                out=gram_diagonal[:],
-                in0=gram[:].rearrange("p (m n) -> p m n", m=TOKEN_TILES),
-                in1=ident_scaled[:].unsqueeze(1).to_broadcast([P, TOKEN_TILES, P]),
-                op=ALU.mult,
-            )
-            nc.vector.tensor_reduce(out=x_sq_scaled[:], in_=gram_diagonal[:], axis=AX.X, op=ALU.add)
-
-        soft = ctx.enter_context(tc.tile_pool(name="soft", bufs=2))
-        results = ctx.enter_context(tc.tile_pool(name="results", bufs=3))
-
+        kept = ctx.enter_context(tc.tile_pool(name="kept", bufs=TOKEN_TILES))
+        results = ctx.enter_context(tc.tile_pool(name="results", bufs=4))
+        soft_1 = ctx.enter_context(tc.tile_pool(name="soft_1", bufs=1))
         probs_codes = {}
         probs_scales = {}
-        for m in range(TOKEN_TILES):
-            tokens = slice(m * P, (m + 1) * P)
-            zl = soft.tile([P, CODES], F32)
-            nc.vector.tensor_tensor(out=zl[:], in0=z_sum[m][:], in1=bias_all[:], op=ALU.add)
-            smooth = soft.tile([P, CODES], F32)
-            nc.scalar.activation(out=smooth[:], in_=zl[:], func=ACT.Exp, scale=-2.0)
-            part_dist = soft.tile([P, CODES], F32)
-            nc.vector.scalar_tensor_tensor(
-                out=part_dist[:],
-                in0=xe_sum[m][:],
-                scalar=-1.0 / DIST_SCALE,
-                in1=emb_sq_scaled[:],
-                op0=ALU.mult,
-                op1=ALU.add,
-            )
-            weighted = soft.tile([P, CODES], F32)
-            nc.vector.scalar_tensor_tensor(
-                out=weighted[:],
-                in0=part_dist[:],
-                scalar=x_sq_scaled[:, m : m + 1],
-                in1=smooth[:],
-                op0=ALU.add,
-                op1=ALU.mult,
-            )
-            neg_logit = soft.tile([P, CODES], F32)
-            nc.vector.tensor_tensor(out=neg_logit[:], in0=weighted[:], in1=zl[:], op=ALU.subtract)
-            neg_top = soft.tile([P, 1], F32)
-            nc.vector.tensor_reduce(out=neg_top[:], in_=neg_logit[:], axis=AX.X, op=ALU.min)
-            prob = soft.tile([P, CODES], F32)
-            row_sum = soft.tile([P, 1], F32)
-            nc.scalar.activation(
-                out=prob[:], in_=neg_logit[:], func=ACT.Exp, scale=-1.0, bias=neg_top[:], accum_out=row_sum[:]
-            )
-            inv_sum = soft.tile([P, 1], F32)
-            nc.vector.reciprocal(out=inv_sum[:], in_=row_sum[:])
-            probs_bf16 = soft.tile([P, CODES], BF16)
-            nc.scalar.activation(out=probs_bf16[:], in_=prob[:], func=ACT.Copy, scale=inv_sum[:])
-            probs = soft.tile([P, CODES], F32)
-            nc.scalar.activation(out=probs[:], in_=prob[:], func=ACT.Copy, scale=inv_sum[:])
-            nc.sync.dma_start(out=out_1[tokens, :], in_=probs[:])
+        with tc.tile_pool(name="soft_0", bufs=1) as soft_0, tc.manual_schedule():
+            zl = {}
+            smooth = {}
+            logit = {}
+            neg_top = {}
+            prob = {}
+            row_sum = {}
+            inv_sum = {}
+            probs_bf16 = {}
+            probs_bank = {}
+            grouped_probs = {}
+            for m, soft in ((0, soft_0), (1, soft_1)):
+                zl[m] = soft.tile([P, CODES], F32, name="zl")
+                smooth[m] = soft.tile([P, CODES], F32, name="smooth")
+                logit[m] = soft.tile([P, CODES], F32, name="logit")
+                neg_top[m] = soft.tile([P, 1], F32, name="neg_top")
+                prob[m] = kept.tile([P, CODES], F32, name="prob")
+                row_sum[m] = soft.tile([P, 1], F32, name="row_sum")
+                inv_sum[m] = kept.tile([P, 1], F32, name="inv_sum")
+                probs_bf16[m] = soft.tile([P, CODES], BF16, name="probs_bf16")
+                grouped_probs[m] = soft.tile([P, P * PACK], BF16, name="grouped_probs", align_bytes=64)
+                probs_codes[m] = kept.tile([P, P], U32, name="probs_codes", align_bytes=64)
+                probs_scales[m] = kept.tile([P, P], U8, name="probs_scales", align_bytes=64)
 
-            probs_bank = banks.tile([P, CODES], BF16, tag="bank")
-            for t in range(CODE_TILES):
-                nc.tensor.transpose(
-                    out=probs_bank[:, t * P : (t + 1) * P],
-                    in_=probs_bf16[:, t * P : (t + 1) * P],
-                    identity=ident_bf16[:],
+            def add_bias(m):
+                nc.vector.tensor_tensor(out=zl[m][:], in0=z_sum[m][:], in1=bias_all[:], op=ALU.add)
+                nc.scalar.activation(out=smooth[m][:], in_=zl[m][:], func=ACT.Exp, scale=-2.0)
+
+            def part_distance(m):
+                nc.vector.scalar_tensor_tensor(
+                    out=logit[m][:],
+                    in0=xe_sum[m][:],
+                    scalar=-1.0 / DIST_SCALE,
+                    in1=emb_sq_scaled[:],
+                    op0=ALU.mult,
+                    op1=ALU.add,
                 )
-            grouped_probs = soft.tile([P, P * PACK], BF16, align_bytes=64)
-            nc.scalar.copy(
-                out=grouped_probs[:].rearrange("p (r t) -> p r t", t=PACK),
-                in_=probs_bank[:].rearrange("p (t r) -> p r t", t=PACK),
-            )
-            probs_codes[m] = soft.tile([P, P], U32, name="probs_codes", align_bytes=64)
-            probs_scales[m] = soft.tile([P, P], U8, name="probs_scales", align_bytes=64)
-            quantise(probs_codes[m][:], probs_scales[m][:], grouped_probs[:])
+
+            def weigh(m):
+                nc.vector.scalar_tensor_tensor(
+                    out=logit[m][:],
+                    in0=logit[m][:],
+                    scalar=x_sq_scaled[:, m : m + 1],
+                    in1=smooth[m][:],
+                    op0=ALU.add,
+                    op1=ALU.mult,
+                )
+
+            def negate_logit(m):
+                nc.vector.tensor_tensor(out=logit[m][:], in0=logit[m][:], in1=zl[m][:], op=ALU.subtract)
+
+            def find_top(m):
+                nc.vector.tensor_reduce(out=neg_top[m][:], in_=logit[m][:], axis=AX.X, op=ALU.min)
+
+            def exponentiate(m):
+                nc.scalar.activation(
+                    out=prob[m][:],
+                    in_=logit[m][:],
+                    func=ACT.Exp,
+                    scale=-1.0,
+                    bias=neg_top[m][:],
+                    accum_out=row_sum[m][:],
+                )
+
+            def scale_probs(m, out):
+                nc.vector.tensor_scalar(out=out, in0=prob[m][:], scalar1=inv_sum[m][:], scalar2=None, op0=ALU.mult)
+
+            def round_probs(m):
+                nc.vector.reciprocal(out=inv_sum[m][:], in_=row_sum[m][:])
+                scale_probs(m, probs_bf16[m][:])
+
+            def turn_probs(m):
+                probs_bank[m] = banks.tile([P, CODES], BF16, tag="bank", name="probs_bank")
+                for t in range(CODE_TILES):
+                    nc.tensor.transpose(
+                        out=probs_bank[m][:, t * P : (t + 1) * P],
+                        in_=probs_bf16[m][:, t * P : (t + 1) * P],
+                        identity=ident_bf16[:],
+                    )
+
+            def group_probs(m):
+                nc.scalar.copy(
+                    out=grouped_probs[m][:].rearrange("p (r t) -> p r t", t=PACK),
+                    in_=probs_bank[m][:].rearrange("p (t r) -> p r t", t=PACK),
+                )
+
+            def quantise_probs(m):
+                quantise(probs_codes[m][:], probs_scales[m][:], grouped_probs[m][:])
+
+            def store_probs(m):
+                probs = kept.tile([P, CODES], F32, name="probs")
+                scale_probs(m, probs[:])
+                nc.sync.dma_start(out=out_1[m * P : (m + 1) * P, :], in_=probs[:])
+
+            add_bias(0)
+            part_distance(0)
+            add_bias(1)
+            weigh(0)
+            negate_logit(0)
+            find_top(0)
+            exponentiate(0)
+            part_distance(1)
+            weigh(1)
+            round_probs(0)
+            turn_probs(0)
+            negate_logit(1)
+            find_top(1)
+            group_probs(0)
+            quantise_probs(0)
+            exponentiate(1)
+            round_probs(1)
+            turn_probs(1)
+            group_probs(1)
+            quantise_probs(1)
+
+        by_code_late = ctx.enter_context(tc.tile_pool(name="by_code_late", bufs=2))
 
         result = {}
-        for j in range(PASSES):
-            if j >= EARLY_BLOCKS:
-                quantise_emb_by_code(j, regroup_emb_by_code(j))
+        made = []
+
+        def product(j, m):
             cols = slice(j * K_PASS, (j + 1) * K_PASS)
-            place = j % STORE_BLOCKS
-            for m in range(TOKEN_TILES):
-                if place == 0:
-                    result[m] = results.tile([P, STORE_BLOCKS * BANK], F32, name="result%d" % m)
-                bank = sums.tile([P, BANK], F32, tag=sum_tags[(TOKEN_TILES * j + m) % len(sum_tags)], name="product")
-                nc.tensor.matmul_mx(
-                    out=bank[:],
-                    lhsT=probs_codes[m][:].bitcast(FP8X4),
-                    lhsT_scale=probs_scales[m][:],
-                    rhs=emb_by_code[:, cols].bitcast(FP8X4),
-                    rhs_scale=emb_by_code_scales[:, cols],
-                    start=True,
-                    stop=True,
+            place = 0 if j < SINGLE_BLOCKS else j % STORE_BLOCKS
+            if place == 0:
+                result[m] = results.tile([P, STORE_BLOCKS * BANK], F32, name="result%d" % m)
+            bank = sums.tile([P, BANK], F32, tag=sum_tags[len(made) % len(sum_tags)], name="product")
+            made.append(bank)
+            nc.tensor.matmul_mx(
+                out=bank[:],
+                lhsT=probs_codes[m][:].bitcast(FP8X4),
+                lhsT_scale=probs_scales[m][:],
+                rhs=emb_by_code[:, cols].bitcast(FP8X4),
+                rhs_scale=emb_by_code_scales[:, cols],
+                start=True,
+                stop=True,
+            )
+            engine_copy = nc.vector.tensor_copy if j >= PASSES - VECTOR_BLOCKS and m == 1 else nc.scalar.copy
+            engine_copy(out=result[m][:, place * BANK : (place + 1) * BANK], in_=bank[:])
+            if j < SINGLE_BLOCKS or place == STORE_BLOCKS - 1:
+                first = (j - place) * K_PASS
+                nc.sync.dma_start(
+                    out=out_0[m * P : (m + 1) * P, first : first + (place + 1) * BANK],
+                    in_=result[m][:, 0 : (place + 1) * BANK],
                 )
-                nc.scalar.copy(out=result[m][:, place * BANK : (place + 1) * BANK], in_=bank[:])
-                if place == STORE_BLOCKS - 1:
-                    first = (j - place) * K_PASS
-                    nc.sync.dma_start(
-                        out=out_0[m * P : (m + 1) * P, first : first + STORE_BLOCKS * BANK], in_=result[m][:]
-                    )
+
+        for m in range(TOKEN_TILES):
+            for j in range(EARLY_BLOCKS):
+                product(j, m)
+            store_probs(m)
+        for j in range(EARLY_BLOCKS, PASSES):
+            quantise_emb_by_code(j, regroup_emb_by_code(j, by_code_late))
+            for m in range(TOKEN_TILES):
+                product(j, m)

@@ -25,10 +25,9 @@ CHUNKS = FEATURES // CHUNK
 PASSES_PER_CHUNK = CHUNK // K_PASS
 BANK = 512
 AHEAD = 2
-EARLY_BLOCKS = 6
+EARLY_BLOCKS = 8
 EARLY_EVERY = 2
 SINGLE_BLOCKS = 2
-VECTOR_BLOCKS = 2
 STORE_BLOCKS = 2
 DIST_SCALE = 400.0
 SCALAR_EMPTIES_EVERY = 2
@@ -291,8 +290,10 @@ def tile_vq_payam_gssoft_pa_k_kernel(tc, x, logvar_W, logvar_b, embedding, out_0
                     )
                 nc.scalar.activation(out=emb_sq_scaled[:], in_=emb_sq_bank[:], func=ACT.Copy, scale=0.5 / DIST_SCALE)
 
+            load_emb(0, 0, PASSES_PER_CHUNK)
+            load_w(0, 0, PASSES_PER_CHUNK)
             load_x(0)
-            for part in range(PASSES_PER_CHUNK):
+            for part in range(1, PASSES_PER_CHUNK):
                 load_emb(0, part, PASSES_PER_CHUNK)
                 load_w(0, part, PASSES_PER_CHUNK)
             for c in range(1, AHEAD):
@@ -317,19 +318,18 @@ def tile_vq_payam_gssoft_pa_k_kernel(tc, x, logvar_W, logvar_b, embedding, out_0
                 grouped_x, grouped_emb = empty_banks(last)
                 operands[last] = quantise_x_and_w(grouped_x, grouped_w)
                 add_gram(last, grouped_x)
-                sum_embedding_squares()
                 for m in range(TOKEN_TILES):
                     multiply(last, m, z_sum, *operands[last][2:4])
-                emb_operand = quantise_emb(grouped_emb)
-                for m in range(TOKEN_TILES):
-                    multiply(last, m, xe_sum, *emb_operand)
                 nc.vector.tensor_tensor(
                     out=gram_diagonal[:],
                     in0=gram[:].rearrange("p (m n) -> p m n", m=TOKEN_TILES),
                     in1=ident_scaled[:].unsqueeze(1).to_broadcast([P, TOKEN_TILES, P]),
                     op=ALU.mult,
                 )
-                nc.vector.tensor_reduce(out=x_sq_scaled[:], in_=gram_diagonal[:], axis=AX.X, op=ALU.add)
+                sum_embedding_squares()
+                emb_operand = quantise_emb(grouped_emb)
+                for m in range(TOKEN_TILES):
+                    multiply(last, m, xe_sum, *emb_operand)
 
         kept = ctx.enter_context(tc.tile_pool(name="kept", bufs=TOKEN_TILES))
         results = ctx.enter_context(tc.tile_pool(name="results", bufs=4))
@@ -432,15 +432,16 @@ def tile_vq_payam_gssoft_pa_k_kernel(tc, x, logvar_W, logvar_b, embedding, out_0
 
             add_bias(0)
             part_distance(0)
-            add_bias(1)
+            nc.vector.tensor_reduce(out=x_sq_scaled[:], in_=gram_diagonal[:], axis=AX.X, op=ALU.add)
             weigh(0)
             negate_logit(0)
             find_top(0)
             exponentiate(0)
+            add_bias(1)
             part_distance(1)
-            weigh(1)
             round_probs(0)
             turn_probs(0)
+            weigh(1)
             negate_logit(1)
             find_top(1)
             group_probs(0)
@@ -472,8 +473,7 @@ def tile_vq_payam_gssoft_pa_k_kernel(tc, x, logvar_W, logvar_b, embedding, out_0
                 start=True,
                 stop=True,
             )
-            engine_copy = nc.vector.tensor_copy if j >= PASSES - VECTOR_BLOCKS and m == 1 else nc.scalar.copy
-            engine_copy(out=result[m][:, place * BANK : (place + 1) * BANK], in_=bank[:])
+            nc.scalar.copy(out=result[m][:, place * BANK : (place + 1) * BANK], in_=bank[:])
             if j < SINGLE_BLOCKS or place == STORE_BLOCKS - 1:
                 first = (j - place) * K_PASS
                 nc.sync.dma_start(

from contextlib import ExitStack

import concourse.mybir as mybir
from concourse.masks import make_identity

F32 = mybir.dt.float32
BF16 = mybir.dt.bfloat16
U32 = mybir.dt.uint32
U8 = mybir.dt.uint8
FP8X4 = mybir.dt.float8_e4m3fn_x4
ACT = mybir.ActivationFunctionType
ALU = mybir.AluOpType
AX = mybir.AxisListType

P = 128
PACK = 4
K_PASS = P * PACK
TOKENS, FEATURES, CODES = 256, 8192, 512
TOKEN_TILES = TOKENS // P
CODE_TILES = CODES // P
PASSES = FEATURES // K_PASS
PAIRS = K_PASS // 2
CHUNK = 1024
CHUNKS = FEATURES // CHUNK
PASSES_PER_CHUNK = CHUNK // K_PASS
BANK = 512
AHEAD = 2
EARLY_BLOCKS = 8
EARLY_EVERY = 2
SINGLE_BLOCKS = 2
STORE_BLOCKS = 2
DIST_SCALE = 400.0
SCALAR_EMPTIES_EVERY = 2

FLOPS = 3 * 2 * TOKENS * FEATURES * CODES


def tile_vq_payam_gssoft_pa_k_kernel(tc, x, logvar_W, logvar_b, embedding, out_0, out_1):
    nc = tc.nc

    x_view = x.rearrange("(m p) f -> p m f", p=P)
    emb_view = embedding.rearrange("(t p) f -> p t f", p=P)
    w_view = logvar_W.rearrange("(s q e) n -> q s e n", q=P, e=2)

    with ExitStack() as ctx:
        consts = ctx.enter_context(tc.tile_pool(name="consts", bufs=1))
        keep = ctx.enter_context(tc.tile_pool(name="keep", bufs=1))
        by_code = ctx.enter_context(tc.tile_pool(name="by_code", bufs=2))
        sums = ctx.enter_context(tc.psum_pool(name="sums", bufs=1))
        banks = ctx.enter_context(tc.psum_pool(name="banks", bufs=3))

        ident_f32 = consts.tile([P, P], F32)
        make_identity(nc, ident_f32[:])
        ident_bf16 = consts.tile([P, P], BF16)
        make_identity(nc, ident_bf16[:])

        warm_in = consts.tile([P, 1], F32)
        nc.vector.memset(warm_in[:], 0.0)
        warm_out = consts.tile([P, 1], F32)
        nc.scalar.activation(out=warm_out[:], in_=warm_in[:], func=ACT.Exp)

        bias_all = consts.tile([P, CODES], BF16)

        emb_sq_parts = consts.tile([P, CODE_TILES * (CHUNKS + 1)], F32)
        gram_diagonal = consts.tile([P, TOKEN_TILES, P], F32)
        emb_sq = consts.tile([P, CODE_TILES], F32)
        ident_scaled = consts.tile([P, P], F32)
        nc.vector.tensor_scalar(
            out=ident_scaled[:], in0=ident_f32[:], scalar1=0.5 / DIST_SCALE, scalar2=None, op0=ALU.mult
        )
        x_sq_scaled = consts.tile([P, TOKEN_TILES], F32)
        emb_sq_scaled = consts.tile([P, CODES], F32)

        raw_emb = {}
        emb_rows = {}
        for c in range(CHUNKS):
            parts = PASSES_PER_CHUNK if c == 0 else 1
            for part in range(parts):
                raw_emb[c, part] = keep.tile([P, CODE_TILES * CHUNK // parts], BF16, name="raw_emb%d_%d" % (c, part))
            for part in range(PASSES_PER_CHUNK):
                rows = raw_emb[c, part % parts][:].rearrange("p (t f) -> p t f", t=CODE_TILES)
                first = (part // parts) * K_PASS
                emb_rows[c * PASSES_PER_CHUNK + part] = rows[:, :, first : first + K_PASS]
        emb_by_code = keep.tile([P, FEATURES], U32, align_bytes=64)
        emb_by_code_scales = keep.tile([P, FEATURES], U8, align_bytes=64)

        z_sum = {}
        xe_sum = {}
        gram = sums.tile([P, TOKENS], F32, name="gram")
        sum_tags = []
        for m in range(TOKEN_TILES):
            z_sum[m] = sums.tile([P, BANK], F32, name="z_sum%d" % m)
            xe_sum[m] = sums.tile([P, BANK], F32, name="xe_sum%d" % m)
            sum_tags.extend(["z_sum%d" % m, "xe_sum%d" % m])
        sum_tags.append("gram")
        zeros = consts.tile([P, TOKENS], BF16)
        nc.vector.memset(zeros[:], 0.0)

        def quantise(codes, scales, grouped):
            nc.vector.quantize_mx(out=codes.bitcast(FP8X4), scales=scales, in_=grouped)

        def regroup(grouped, rows):
            nc.vector.tensor_copy(
                out=grouped.rearrange("p (c i t) -> p c t i", i=4, t=PACK),
                in_=rows.rearrange("p t (c i) -> p c t i", i=4),
            )

        def regroup_emb_by_code(j, pool):
            grouped = pool.tile([P, K_PASS * PACK], BF16, name="grouped_by_code", align_bytes=64)
            regroup(grouped[:], emb_rows[j])
            return grouped

        def quantise_emb_by_code(j, grouped):
            cols = slice(j * K_PASS, (j + 1) * K_PASS)
            quantise(emb_by_code[:, cols], emb_by_code_scales[:, cols], grouped[:])

        with ExitStack() as stream:
            x_pool = stream.enter_context(tc.tile_pool(name="x_pool", bufs=AHEAD + 1))
            w_pool = stream.enter_context(tc.tile_pool(name="w_pool", bufs=AHEAD + 1))
            grouped_pool = stream.enter_context(tc.tile_pool(name="grouped_pool", bufs=2))
            codes_pool = stream.enter_context(tc.tile_pool(name="codes_pool", bufs=3))
            unread = stream.enter_context(tc.tile_pool(name="unread", bufs=2))

            x_rows = {}
            raw_w = {}
            turned = {}
            operands = {}

            def load_x(c):
                tile = x_pool.tile([P, TOKEN_TILES * CHUNK], BF16, name="raw_x")
                rows = tile[:].rearrange("p (m f) -> p m f", m=TOKEN_TILES)
                nc.sync.dma_start(out=rows, in_=x_view[:, :, c * CHUNK : (c + 1) * CHUNK])
                for part in range(PASSES_PER_CHUNK):
                    x_rows[c * PASSES_PER_CHUNK + part] = rows[:, :, part * K_PASS : (part + 1) * K_PASS]

            def load_w(c, part, parts):
                if part == 0:
                    raw_w[c] = w_pool.tile([P, PASSES_PER_CHUNK * PACK * CODES], BF16, name="raw_w")
                halves = raw_w[c][:].rearrange("p (s e n) -> p s e n", e=2, n=CODES)
                count = 2 * PASSES_PER_CHUNK // parts
                first = 2 * c * PASSES_PER_CHUNK + part * count
                nc.sync.dma_start(
                    out=halves[:, part * count : (part + 1) * count, :, :], in_=w_view[:, first : first + count, :, :]
                )

            def load_emb(c, part, parts):
                width = CHUNK // parts
                first = c * CHUNK + part * width
                nc.sync.dma_start(
                    out=raw_emb[c, part][:].rearrange("p (t f) -> p t f", t=CODE_TILES),
                    in_=emb_view[:, :, first : first + width],
                )

            def load_chunk(c):
                load_x(c)
                load_w(c, 0, 1)
                load_emb(c, 0, 1)

            def square_rows(k):
                c, half = divmod(k, 2)
                if c == 0:
                    tile, width, tiles = raw_emb[0, half], K_PASS, range(CODE_TILES)
                else:
                    tile, width, tiles = raw_emb[c, 0], CHUNK, range(2 * half, 2 * half + 2)
                for t in tiles:
                    squares = unread.tile([P, CHUNK], BF16, name="squares")
                    column = t * (CHUNKS + 1) + (half if c == 0 else c + 1)
                    nc.scalar.activation(
                        out=squares[:, 0:width],
                        in_=tile[:, t * width : (t + 1) * width],
                        func=ACT.Square,
                        accum_out=emb_sq_parts[:, column : column + 1],
                    )

            def transpose_pass(g):
                turned[g] = []
                for rows, first_tile in ((x_rows[g], 0), (emb_rows[g], 0), (emb_rows[g], 2)):
                    bank = banks.tile([P, BANK], F32, tag="bank", name="turned")
                    for i in range(2):
                        words = rows[:, first_tile + i, :].bitcast(F32)
                        for u in range(2):
                            nc.tensor.transpose(
                                out=bank[:, (2 * i + u) * P : (2 * i + u + 1) * P],
                                in_=words[:, u * P : (u + 1) * P],
                                identity=ident_f32[:],
                            )
                    turned[g].append(bank)

            def interleave(engine_copy, grouped_words, bank):
                engine_copy(
                    out=grouped_words.rearrange("p (i r u) -> p i r u", i=2, u=2),
                    in_=bank[:].rearrange("p (i u r) -> p i r u", i=2, u=2),
                )

            def empty_banks(g):
                x_bank, emb_bank_0, emb_bank_1 = turned[g]
                grouped_x = grouped_pool.tile([P, TOKENS * PACK], BF16, bufs=3, align_bytes=64)
                scalar_turn = g % SCALAR_EMPTIES_EVERY == 0
                interleave(nc.scalar.copy if scalar_turn else nc.vector.tensor_copy, grouped_x[:].bitcast(F32), x_bank)
                grouped_emb = grouped_pool.tile([P, CODES * PACK], BF16, align_bytes=64)
                emb_words = grouped_emb[:].bitcast(F32)
                interleave(nc.scalar.copy, emb_words[:, 0:BANK], emb_bank_0)
                interleave(nc.scalar.copy, emb_words[:, BANK : 2 * BANK], emb_bank_1)
                return grouped_x, grouped_emb

            def regroup_w(g):
                c, part = divmod(g, PASSES_PER_CHUNK)
                grouped_w = grouped_pool.tile([P, CODES * PACK], BF16, align_bytes=64)
                w_rows = raw_w[c][:].rearrange("p (g t n) -> p g t n", t=PACK, n=CODES)
                regroup(grouped_w[:], w_rows[:, part, :, :])
                return grouped_w

            def quantise_x_and_w(grouped_x, grouped_w):
                x_codes = codes_pool.tile([P, TOKENS], U32, align_bytes=64)
                x_scales = codes_pool.tile([P, TOKENS], U8, align_bytes=64)
                quantise(x_codes[:], x_scales[:], grouped_x[:])
                w_codes = codes_pool.tile([P, CODES], U32, align_bytes=64)
                w_scales = codes_pool.tile([P, CODES], U8, align_bytes=64)
                quantise(w_codes[:], w_scales[:], grouped_w[:])
                return x_codes, x_scales, w_codes, w_scales

            def quantise_emb(grouped_emb):
                emb_codes = codes_pool.tile([P, CODES], U32, align_bytes=64)
                emb_scales = codes_pool.tile([P, CODES], U8, align_bytes=64)
                quantise(emb_codes[:], emb_scales[:], grouped_emb[:])
                return emb_codes, emb_scales

            def quantise_pass(g):
                grouped_x, grouped_emb = empty_banks(g)
                if g == 0:
                    square_rows(0)
                square_rows(g + 1)
                grouped_w = regroup_w(g)
                early = g % EARLY_EVERY == 0 and g // EARLY_EVERY < EARLY_BLOCKS
                if early:
                    grouped_by_code = regroup_emb_by_code(g // EARLY_EVERY, by_code)
                codes = quantise_x_and_w(grouped_x, grouped_w)
                if early:
                    quantise_emb_by_code(g // EARLY_EVERY, grouped_by_code)
                operands[g] = codes + quantise_emb(grouped_emb) + (grouped_x,)

            def multiply(g, m, total, codes, scales):
                x_codes, x_scales = operands[g][0:2]
                tokens = slice(m * P, (m + 1) * P)
                nc.tensor.matmul_mx(
                    out=total[m][:],
                    lhsT=x_codes[:, tokens].bitcast(FP8X4),
                    lhsT_scale=x_scales[:, tokens],
                    rhs=codes[:].bitcast(FP8X4),
                    rhs_scale=scales[:],
                    start=(g == 0),
                    stop=(g == PASSES - 1),
                )

            def multiply_pass(g):
                w_codes, w_scales, emb_codes, emb_scales, grouped_x = operands[g][2:]
                for m in range(TOKEN_TILES):
                    multiply(g, m, z_sum, w_codes, w_scales)
                    multiply(g, m, xe_sum, emb_codes, emb_scales)
                add_gram(g, grouped_x)

            def add_gram(g, grouped_x):
                if g == 0:
                    nc.tensor.matmul(out=gram[:], lhsT=zeros[:, 0:P], rhs=zeros[:], start=True, stop=False)
                planes = grouped_x[:].rearrange("p (r t) -> p t r", t=PACK)
                for m in range(TOKEN_TILES):
                    for t in range(PACK):
                        plane = planes[:, t, m * P : (m + 1) * P]
                        nc.tensor.matmul(
                            out=gram[:, m * P : (m + 1) * P],
                            lhsT=plane,
                            rhs=plane,
                            start=False,
                            stop=(g == PASSES - 1 and m == TOKEN_TILES - 1 and t == PACK - 1),
                        )

            def sum_embedding_squares():
                nc.vector.tensor_reduce(
                    out=emb_sq[:],
                    in_=emb_sq_parts[:].rearrange("p (t c) -> p t c", t=CODE_TILES),
                    axis=AX.X,
                    op=ALU.add,
                )
                emb_sq_bank = banks.tile([P, BANK], F32, tag="bank")
                for t in range(CODE_TILES):
                    nc.tensor.transpose(
                        out=emb_sq_bank[:, t * P : (t + 1) * P],
                        in_=emb_sq[:, t : t + 1].to_broadcast([P, P]),
                        identity=ident_f32[:],
                    )
                nc.scalar.activation(out=emb_sq_scaled[:], in_=emb_sq_bank[:], func=ACT.Copy, scale=0.5 / DIST_SCALE)

            load_emb(0, 0, PASSES_PER_CHUNK)
            load_w(0, 0, PASSES_PER_CHUNK)
            load_x(0)
            for part in range(1, PASSES_PER_CHUNK):
                load_emb(0, part, PASSES_PER_CHUNK)
                load_w(0, part, PASSES_PER_CHUNK)
            for c in range(1, AHEAD):
                load_chunk(c)
            transpose_pass(0)
            for g in range(PASSES):
                c, part = divmod(g, PASSES_PER_CHUNK)
                if part == 0 and c + AHEAD < CHUNKS:
                    load_chunk(c + AHEAD)
                    if c + AHEAD == CHUNKS - 1:
                        nc.sync.dma_start(out=bias_all[:], in_=logvar_b.partition_broadcast(P))
                if g > 0:
                    multiply_pass(g - 1)
                if g + 1 < PASSES:
                    transpose_pass(g + 1)
                if g < PASSES - 1:
                    quantise_pass(g)

            with tc.manual_schedule():
                last = PASSES - 1
                grouped_w = regroup_w(last)
                grouped_x, grouped_emb = empty_banks(last)
                operands[last] = quantise_x_and_w(grouped_x, grouped_w)
                add_gram(last, grouped_x)
                for m in range(TOKEN_TILES):
                    multiply(last, m, z_sum, *operands[last][2:4])
                nc.vector.tensor_tensor(
                    out=gram_diagonal[:],
                    in0=gram[:].rearrange("p (m n) -> p m n", m=TOKEN_TILES),
                    in1=ident_scaled[:].unsqueeze(1).to_broadcast([P, TOKEN_TILES, P]),
                    op=ALU.mult,
                )
                sum_embedding_squares()
                emb_operand = quantise_emb(grouped_emb)
                for m in range(TOKEN_TILES):
                    multiply(last, m, xe_sum, *emb_operand)

        kept = ctx.enter_context(tc.tile_pool(name="kept", bufs=TOKEN_TILES))
        results = ctx.enter_context(tc.tile_pool(name="results", bufs=4))
        soft_1 = ctx.enter_context(tc.tile_pool(name="soft_1", bufs=1))
        probs_codes = {}
        probs_scales = {}
        with tc.tile_pool(name="soft_0", bufs=1) as soft_0, tc.manual_schedule():
            zl = {}
            smooth = {}
            logit = {}
            neg_top = {}
            prob = {}
            row_sum = {}
            inv_sum = {}
            probs_bf16 = {}
            probs_bank = {}
            grouped_probs = {}
            for m, soft in ((0, soft_0), (1, soft_1)):
                zl[m] = soft.tile([P, CODES], F32, name="zl")
                smooth[m] = soft.tile([P, CODES], F32, name="smooth")
                logit[m] = soft.tile([P, CODES], F32, name="logit")
                neg_top[m] = soft.tile([P, 1], F32, name="neg_top")
                prob[m] = kept.tile([P, CODES], F32, name="prob")
                row_sum[m] = soft.tile([P, 1], F32, name="row_sum")
                inv_sum[m] = kept.tile([P, 1], F32, name="inv_sum")
                probs_bf16[m] = soft.tile([P, CODES], BF16, name="probs_bf16")
                grouped_probs[m] = soft.tile([P, P * PACK], BF16, name="grouped_probs", align_bytes=64)
                probs_codes[m] = kept.tile([P, P], U32, name="probs_codes", align_bytes=64)
                probs_scales[m] = kept.tile([P, P], U8, name="probs_scales", align_bytes=64)

            def add_bias(m):
                nc.vector.tensor_tensor(out=zl[m][:], in0=z_sum[m][:], in1=bias_all[:], op=ALU.add)
                nc.scalar.activation(out=smooth[m][:], in_=zl[m][:], func=ACT.Exp, scale=-2.0)

            def part_distance(m):
                nc.vector.scalar_tensor_tensor(
                    out=logit[m][:],
                    in0=xe_sum[m][:],
                    scalar=-1.0 / DIST_SCALE,
                    in1=emb_sq_scaled[:],
                    op0=ALU.mult,
                    op1=ALU.add,
                )

            def weigh(m):
                nc.vector.scalar_tensor_tensor(
                    out=logit[m][:],
                    in0=logit[m][:],
                    scalar=x_sq_scaled[:, m : m + 1],
                    in1=smooth[m][:],
                    op0=ALU.add,
                    op1=ALU.mult,
                )

            def negate_logit(m):
                nc.vector.tensor_tensor(out=logit[m][:], in0=logit[m][:], in1=zl[m][:], op=ALU.subtract)

            def find_top(m):
                nc.vector.tensor_reduce(out=neg_top[m][:], in_=logit[m][:], axis=AX.X, op=ALU.min)

            def exponentiate(m):
                nc.scalar.activation(
                    out=prob[m][:],
                    in_=logit[m][:],
                    func=ACT.Exp,
                    scale=-1.0,
                    bias=neg_top[m][:],
                    accum_out=row_sum[m][:],
                )

            def scale_probs(m, out):
                nc.vector.tensor_scalar(out=out, in0=prob[m][:], scalar1=inv_sum[m][:], scalar2=None, op0=ALU.mult)

            def round_probs(m):
                nc.vector.reciprocal(out=inv_sum[m][:], in_=row_sum[m][:])
                scale_probs(m, probs_bf16[m][:])

            def turn_probs(m):
                probs_bank[m] = banks.tile([P, CODES], BF16, tag="bank", name="probs_bank")
                for t in range(CODE_TILES):
                    nc.tensor.transpose(
                        out=probs_bank[m][:, t * P : (t + 1) * P],
                        in_=probs_bf16[m][:, t * P : (t + 1) * P],
                        identity=ident_bf16[:],
                    )

            def group_probs(m):
                nc.scalar.copy(
                    out=grouped_probs[m][:].rearrange("p (r t) -> p r t", t=PACK),
                    in_=probs_bank[m][:].rearrange("p (t r) -> p r t", t=PACK),
                )

            def quantise_probs(m):
                quantise(probs_codes[m][:], probs_scales[m][:], grouped_probs[m][:])

            def store_probs(m):
                probs = kept.tile([P, CODES], F32, name="probs")
                scale_probs(m, probs[:])
                nc.sync.dma_start(out=out_1[m * P : (m + 1) * P, :], in_=probs[:])

            add_bias(0)
            part_distance(0)
            nc.vector.tensor_reduce(out=x_sq_scaled[:], in_=gram_diagonal[:], axis=AX.X, op=ALU.add)
            weigh(0)
            negate_logit(0)
            find_top(0)
            exponentiate(0)
            add_bias(1)
            part_distance(1)
            round_probs(0)
            turn_probs(0)
            weigh(1)
            negate_logit(1)
            find_top(1)
            group_probs(0)
            quantise_probs(0)
            exponentiate(1)
            round_probs(1)
            turn_probs(1)
            group_probs(1)
            quantise_probs(1)

        by_code_late = ctx.enter_context(tc.tile_pool(name="by_code_late", bufs=2))

        result = {}
        made = []

        def product(j, m):
            cols = slice(j * K_PASS, (j + 1) * K_PASS)
            place = 0 if j < SINGLE_BLOCKS else j % STORE_BLOCKS
            if place == 0:
                result[m] = results.tile([P, STORE_BLOCKS * BANK], F32, name="result%d" % m)
            bank = sums.tile([P, BANK], F32, tag=sum_tags[len(made) % len(sum_tags)], name="product")
            made.append(bank)
            nc.tensor.matmul_mx(
                out=bank[:],
                lhsT=probs_codes[m][:].bitcast(FP8X4),
                lhsT_scale=probs_scales[m][:],
                rhs=emb_by_code[:, cols].bitcast(FP8X4),
                rhs_scale=emb_by_code_scales[:, cols],
                start=True,
                stop=True,
            )
            nc.scalar.copy(out=result[m][:, place * BANK : (place + 1) * BANK], in_=bank[:])
            if j < SINGLE_BLOCKS or place == STORE_BLOCKS - 1:
                first = (j - place) * K_PASS
                nc.sync.dma_start(
                    out=out_0[m * P : (m + 1) * P, first : first + (place + 1) * BANK],
                    in_=result[m][:, 0 : (place + 1) * BANK],
                )

        for m in range(TOKEN_TILES):
            for j in range(EARLY_BLOCKS):
                product(j, m)
            store_probs(m)
        for j in range(EARLY_BLOCKS, PASSES):
            quantise_emb_by_code(j, regroup_emb_by_code(j, by_code_late))
            for m in range(TOKEN_TILES):
                product(j, m)
